import numpy as np
import ml_dtypes


def mxq(x, axis, fmt="e4m3"):
    dtype, down = {"e4m3": (ml_dtypes.float8_e4m3fn, 7), "e5m2": (ml_dtypes.float8_e5m2, 14)}[fmt]
    v = np.moveaxis(np.asarray(x, np.float32).astype(ml_dtypes.bfloat16).astype(np.float64), axis, -1)
    blocks = v.reshape(v.shape[:-1] + (-1, 32))
    amax = np.abs(blocks).max(-1, keepdims=True)
    byte = np.maximum(np.where(amax > 0, np.frexp(amax)[1] - 1 + 127, 0) - down, 1)
    scale = np.exp2(byte - 127.0)
    codes = (blocks / scale).astype(np.float32).astype(dtype).astype(np.float64)
    return np.moveaxis((codes * scale).reshape(v.shape), -1, axis)


BF16 = ml_dtypes.bfloat16


def bf(x):
    return np.asarray(x, np.float32).astype(BF16)


def f64(x):
    return np.asarray(x).astype(np.float64)


N, D, R = 2048, 512, 4
EPS = 1e-12


def setup_inputs():
    mean = 0.6 * np.random.standard_normal((1, D))
    basis = np.random.standard_normal((R, D)) / np.sqrt(R)
    coef = np.random.standard_normal((N, R))
    low = (coef[:, :, None] * basis[None, :, :]).sum(1)
    return {"x": bf(mean + low + 0.5 * np.random.standard_normal((N, D)))}


def reference(x):
    x = f64(x)
    norm = np.sqrt((x * x).sum(1, keepdims=True))
    xn = x / np.maximum(norm, EPS)
    xq = mxq(xn, 1, "e4m3")
    s = xq @ xq.T
    e = np.exp(s - s.max(1, keepdims=True))
    return (mxq(e, 1, "e4m3") @ mxq(x, 0, "e4m3")) / e.sum(1, keepdims=True)

@@ -1,0 +1,289 @@
+from contextlib import ExitStack
+
+import concourse.mybir as mybir
+from concourse.masks import make_identity
+
+F32 = mybir.dt.float32
+BF16 = mybir.dt.bfloat16
+U32 = mybir.dt.uint32
+U8 = mybir.dt.uint8
+FP8X4 = mybir.dt.float8_e4m3fn_x4
+ALU = mybir.AluOpType
+ACT = mybir.ActivationFunctionType
+AX = mybir.AxisListType
+
+P = 128
+N = 2048
+D = 512
+NB = N // P
+NCH = 4
+FLOPS = 2 * 2 * N * N * D
+
+
+def tile_contranorm_pa_kernel(tc, x, out):
+    nc = tc.nc
+    with ExitStack() as ctx:
+        const = ctx.enter_context(tc.tile_pool(name="const", bufs=1))
+        work = ctx.enter_context(tc.tile_pool(name="work", bufs=2))
+        small = ctx.enter_context(tc.tile_pool(name="small", bufs=4))
+        ps_s = ctx.enter_context(tc.psum_pool(name="ps_s", bufs=5))
+        ps_t = ctx.enter_context(tc.psum_pool(name="ps_t", bufs=2))
+        ps_o = ctx.enter_context(tc.psum_pool(name="ps_o", bufs=1))
+        ctx.enter_context(tc.manual_schedule())
+
+        ident = const.tile([P, P], BF16, name="ident")
+        x_sb = const.tile([P, NB, D], BF16, name="x_sb")
+        xc = const.tile([P, N], U32, name="xc", align_bytes=64)
+        xs = const.tile([P, N], U8, name="xs", align_bytes=64)
+        xqc = const.tile([P, 4 * D], U32, name="xqc", align_bytes=64)
+        xqs = const.tile([P, 4 * D], U8, name="xqs", align_bytes=64)
+        xg_a = const.tile([P, 2, D, 4], BF16, name="xg_a", align_bytes=64)
+        xg_b = const.tile([P, 2, D, 4], BF16, name="xg_b", align_bytes=64)
+        ss_s = const.tile([P, 8], F32, name="ss_s")
+        ss_v = const.tile([P, 8], F32, name="ss_v")
+        ssc = const.tile([P, NB], F32, name="ssc")
+        nrm = const.tile([P, NB], F32, name="nrm")
+        rn = const.tile([P, NB], F32, name="rn")
+        one = const.tile([P, 1], F32, name="one")
+        dmy = const.tile([P, 2], F32, name="dmy")
+
+        x_v = x.rearrange("(c p) d -> p c d", p=P)
+        for c in range(NCH):
+            nc.sync.dma_start(out=x_sb[:, 4 * c : 4 * c + 4, :], in_=x_v[:, 4 * c : 4 * c + 4, :])
+
+        nc.vector.memset(one[:], 1.0)
+        make_identity(nc, ident[:])
+        nc.scalar.activation(out=dmy[:, 0:1], in_=one[:], func=ACT.Sqrt)
+
+        xn_t = {}
+        tx_t = {}
+        xng_t = {}
+
+        def sumsq(c):
+            for a in range(2):
+                junk_s = work.tile([P, D], BF16, name="junk_s", tag="junk_s")
+                nc.scalar.activation(
+                    out=junk_s[:], in_=x_sb[:, 4 * c + a, :], func=ACT.Square,
+                    accum_out=ss_s[:, 2 * c + a : 2 * c + a + 1],
+                )
+            for a in range(2):
+                junk_v = work.tile([P, D], F32, name="junk_v", tag="junk_v")
+                nc.vector.scalar_tensor_tensor(
+                    out=junk_v[:], in0=x_sb[:, 4 * c + 2 + a, :], scalar=1.0, in1=x_sb[:, 4 * c + 2 + a, :],
+                    op0=ALU.mult, op1=ALU.mult, accum_out=ss_v[:, 2 * c + a : 2 * c + a + 1],
+                )
+            nc.vector.tensor_scalar_max(out=ssc[:, 4 * c : 4 * c + 2], in0=ss_s[:, 2 * c : 2 * c + 2], scalar1=1e-24)
+            nc.vector.tensor_scalar_max(out=ssc[:, 4 * c + 2 : 4 * c + 4], in0=ss_v[:, 2 * c : 2 * c + 2], scalar1=1e-24)
+
+        def normalise(c):
+            nc.scalar.activation(out=nrm[:, 4 * c : 4 * c + 4], in_=ssc[:, 4 * c : 4 * c + 4], func=ACT.Sqrt)
+            nc.vector.reciprocal(out=rn[:, 4 * c : 4 * c + 4], in_=nrm[:, 4 * c : 4 * c + 4])
+            xn = work.tile([P, 4, D], BF16, name="xn", tag="xn")
+            for a in range(4):
+                nc.vector.tensor_scalar_mul(out=xn[:, a, :], in0=x_sb[:, 4 * c + a, :], scalar1=rn[:, 4 * c + a : 4 * c + a + 1])
+            xn_t[c] = xn
+            for h in range(2):
+                tx = ps_s.tile([P, 2, 4, P], BF16, name="tx", tag="s")
+                for a in range(2):
+                    for t in range(4):
+                        nc.tensor.transpose(tx[:, a, t, :], xn[:, 2 * h + a, t * P : (t + 1) * P], ident[:])
+                tx_t[(c, h)] = tx
+
+        def copy_xn(c, h, eng):
+            if h == 0:
+                xng = work.tile([P, 4, P, 4], BF16, name="xng", tag="xng", align_bytes=64)
+                xng_t[c] = xng
+            dst = xng_t[c][:, 2 * h : 2 * h + 2, :, :]
+            src = tx_t[(c, h)][:].rearrange("p a t r -> p a r t")
+            if eng == "v":
+                nc.vector.tensor_copy(out=dst, in_=src)
+            else:
+                nc.scalar.copy(out=dst, in_=src)
+
+        def quant_xn(c):
+            nc.vector.quantize_mx(
+                out=xc[:, 512 * c : 512 * (c + 1)].bitcast(FP8X4),
+                scales=xs[:, 512 * c : 512 * (c + 1)],
+                in_=xng_t[c][:].rearrange("p a r t -> p (a r t)"),
+            )
+
+        sumsq(0)
+        sumsq(1)
+        normalise(0)
+        sumsq(2)
+        normalise(1)
+        copy_xn(0, 0, "s")
+        copy_xn(0, 1, "s")
+        sumsq(3)
+        normalise(2)
+        quant_xn(0)
+        copy_xn(1, 0, "s")
+        copy_xn(1, 1, "s")
+        normalise(3)
+        quant_xn(1)
+        copy_xn(2, 0, "s")
+        copy_xn(2, 1, "s")
+        copy_xn(3, 0, "v")
+        copy_xn(3, 1, "s")
+        quant_xn(2)
+        quant_xn(3)
+
+        def regroup_x(g, eng):
+            xg = xg_a if g < 2 else xg_b
+            dst = xg[:, g % 2, :, :].rearrange("p (c i) t -> p c t i", i=4)
+            src = x_sb[:, 4 * g : 4 * g + 4, :].rearrange("p t (c i) -> p c t i", i=4)
+            if eng == "v":
+                nc.vector.tensor_copy(out=dst, in_=src)
+            else:
+                nc.scalar.copy(out=dst, in_=src)
+
+        def quant_x(half):
+            xg = xg_a if half == 0 else xg_b
+            nc.vector.quantize_mx(
+                out=xqc[:, 1024 * half : 1024 * (half + 1)].bitcast(FP8X4),
+                scales=xqs[:, 1024 * half : 1024 * (half + 1)],
+                in_=xg[:].rearrange("p g d t -> p (g d t)"),
+            )
+
+        s_t = {}
+        nm_t = {}
+        e_t = {}
+        l4_t = {}
+        rl_t = {}
+        tp_t = {}
+        eg_t = {}
+        ec_t = {}
+        o_t = {}
+
+        def mm1(i, n):
+            s = ps_s.tile([P, 512], F32, name="s", tag="s")
+            nc.tensor.matmul_mx(
+                out=s[:],
+                lhsT=xc[:, i * P : (i + 1) * P].bitcast(FP8X4),
+                lhsT_scale=xs[:, i * P : (i + 1) * P],
+                rhs=xc[:, n * 512 : (n + 1) * 512].bitcast(FP8X4),
+                rhs_scale=xs[:, n * 512 : (n + 1) * 512],
+                start=True,
+                stop=True,
+            )
+            s_t[(i, n)] = s
+
+        def vmax(i):
+            mx4 = small.tile([P, 4], F32, name="mx4", tag="mx4")
+            for n in range(4):
+                nc.vector.tensor_reduce(out=mx4[:, n : n + 1], in_=s_t[(i, n)][:], axis=AX.X, op=ALU.max)
+            nm = small.tile([P, 1], F32, name="nm", tag="nm")
+            nc.vector.tensor_reduce(out=nm[:], in_=mx4[:], axis=AX.X, op=ALU.max, negate=True)
+            nm_t[i] = nm
+
+        def expo(i):
+            e_sb = work.tile([P, N], BF16, name="e_sb", tag="e_sb")
+            l4 = small.tile([P, 4], F32, name="l4", tag="l4")
+            for n in range(4):
+                nc.scalar.activation(
+                    out=e_sb[:, n * 512 : (n + 1) * 512], in_=s_t[(i, n)][:], func=ACT.Exp,
+                    bias=nm_t[i][:, 0:1], scale=1.0, accum_out=l4[:, n : n + 1],
+                )
+            e_t[i] = e_sb
+            l4_t[i] = l4
+
+        def lsum(i):
+            l1 = small.tile([P, 1], F32, name="l1", tag="l1")
+            nc.vector.tensor_reduce(out=l1[:], in_=l4_t[i][:], axis=AX.X, op=ALU.add)
+            rl = small.tile([P, 1], F32, name="rl", tag="rl")
+            nc.vector.reciprocal(out=rl[:], in_=l1[:])
+            rl_t[i] = rl
+
+        def tr(i):
+            for h in range(2):
+                tp = ps_t.tile([P, 2, 4, P], BF16, name="tp", tag="t")
+                for a in range(2):
+                    for t in range(4):
+                        j0 = (2 * h + a) * 512 + t * P
+                        nc.tensor.transpose(tp[:, a, t, :], e_t[i][:, j0 : j0 + P], ident[:])
+                tp_t[(i, h)] = tp
+
+        def co(i, h, eng):
+            if h == 0:
+                eg = work.tile([P, 4, P, 4], BF16, name="eg", tag="eg", align_bytes=64)
+                eg_t[i] = eg
+            dst = eg_t[i][:, 2 * h : 2 * h + 2, :, :]
+            src = tp_t[(i, h)][:].rearrange("p a t r -> p a r t")
+            if eng == "v":
+                nc.vector.tensor_copy(out=dst, in_=src)
+            else:
+                nc.scalar.copy(out=dst, in_=src)
+
+        def quant_e(i):
+            ec = work.tile([P, 512], U32, name="ec", tag="ec", align_bytes=64)
+            es = work.tile([P, 512], U8, name="es", tag="es", align_bytes=64)
+            nc.vector.quantize_mx(
+                out=ec[:].bitcast(FP8X4), scales=es[:], in_=eg_t[i][:].rearrange("p g r t -> p (g r t)")
+            )
+            ec_t[i] = (ec, es)
+
+        def mm2(i, g):
+            if g == 0:
+                o_ps = ps_o.tile([P, D], F32, name="o_ps", tag="o")
+                o_t[i] = o_ps
+            ec, es = ec_t[i]
+            nc.tensor.matmul_mx(
+                out=o_t[i][:],
+                lhsT=ec[:, g * P : (g + 1) * P].bitcast(FP8X4),
+                lhsT_scale=es[:, g * P : (g + 1) * P],
+                rhs=xqc[:, g * D : (g + 1) * D].bitcast(FP8X4),
+                rhs_scale=xqs[:, g * D : (g + 1) * D],
+                start=(g == 0),
+                stop=(g == 3),
+            )
+
+        def fin(i):
+            o_sb = work.tile([P, D], F32, name="o_sb", tag="o_sb", bufs=3)
+            nc.scalar.activation(out=o_sb[:], in_=o_t[i][:], func=ACT.Copy, scale=rl_t[i][:, 0:1])
+            nc.sync.dma_start(out=out[i * P : (i + 1) * P, :], in_=o_sb[:])
+
+        nc.scalar.activation(out=dmy[:, 1:2], in_=one[:], func=ACT.Exp)
+        regroup_x(3, "s")
+
+        for k in range(-1, NB + 2):
+            has_a = 0 <= k + 1 < NB
+            has_k = 0 <= k < NB
+            has_c = 0 <= k - 1 < NB
+            has_b = 0 <= k - 2 < NB
+            if has_c:
+                lsum(k - 1)
+                co(k - 1, 0, "v")
+            if has_k:
+                expo(k)
+            if has_c:
+                co(k - 1, 1, "s")
+            if has_a:
+                mm1(k + 1, 0)
+            if has_b:
+                mm2(k - 2, 0)
+                mm2(k - 2, 1)
+            if has_a:
+                mm1(k + 1, 1)
+            if has_b:
+                mm2(k - 2, 2)
+                mm2(k - 2, 3)
+            if has_a:
+                mm1(k + 1, 2)
+                mm1(k + 1, 3)
+            if k == -1:
+                regroup_x(0, "v")
+            if k == 0:
+                regroup_x(1, "v")
+            if has_a:
+                vmax(k + 1)
+            if k == 0:
+                regroup_x(2, "v")
+                quant_x(0)
+            if has_k:
+                tr(k)
+            if has_c:
+                quant_e(k - 1)
+            if k == 1:
+                quant_x(1)
+            if has_b:
+                fin(k - 2)

@@ -25,10 +25,10 @@ def tile_contranorm_pa_kernel(tc, x, out):
     with ExitStack() as ctx:
         const = ctx.enter_context(tc.tile_pool(name="const", bufs=1))
         work = ctx.enter_context(tc.tile_pool(name="work", bufs=2))
-        small = ctx.enter_context(tc.tile_pool(name="small", bufs=4))
-        ps_s = ctx.enter_context(tc.psum_pool(name="ps_s", bufs=5))
+        small = ctx.enter_context(tc.tile_pool(name="small", bufs=6))
+        ps_s = ctx.enter_context(tc.psum_pool(name="ps_s", bufs=4))
         ps_t = ctx.enter_context(tc.psum_pool(name="ps_t", bufs=2))
-        ps_o = ctx.enter_context(tc.psum_pool(name="ps_o", bufs=1))
+        ps_o = ctx.enter_context(tc.psum_pool(name="ps_o", bufs=2))
         ctx.enter_context(tc.manual_schedule())
 
         ident = const.tile([P, P], BF16, name="ident")
@@ -78,12 +78,17 @@ def tile_contranorm_pa_kernel(tc, x, out):
         def normalise(c):
             nc.scalar.activation(out=nrm[:, 4 * c : 4 * c + 4], in_=ssc[:, 4 * c : 4 * c + 4], func=ACT.Sqrt)
             nc.vector.reciprocal(out=rn[:, 4 * c : 4 * c + 4], in_=nrm[:, 4 * c : 4 * c + 4])
-            xn = work.tile([P, 4, D], BF16, name="xn", tag="xn")
+            xn = work.tile([P, 4, D], BF16, name="xn", tag="xn", bufs=4)
             for a in range(4):
                 nc.vector.tensor_scalar_mul(out=xn[:, a, :], in0=x_sb[:, 4 * c + a, :], scalar1=rn[:, 4 * c + a : 4 * c + a + 1])
             xn_t[c] = xn
             for h in range(2):
-                tx = ps_s.tile([P, 2, 4, P], BF16, name="tx", tag="s")
+                if c < 2:
+                    tx = ps_s.tile([P, 2, 4, P], BF16, name="tx", tag="s")
+                elif c == 2:
+                    tx = ps_t.tile([P, 2, 4, P], BF16, name="tx", tag="t")
+                else:
+                    tx = ps_o.tile([P, 2, 4, P], BF16, name="tx", tag="o")
                 for a in range(2):
                     for t in range(4):
                         nc.tensor.transpose(tx[:, a, t, :], xn[:, 2 * h + a, t * P : (t + 1) * P], ident[:])
@@ -107,27 +112,6 @@ def tile_contranorm_pa_kernel(tc, x, out):
                 in_=xng_t[c][:].rearrange("p a r t -> p (a r t)"),
             )
 
-        sumsq(0)
-        sumsq(1)
-        normalise(0)
-        sumsq(2)
-        normalise(1)
-        copy_xn(0, 0, "s")
-        copy_xn(0, 1, "s")
-        sumsq(3)
-        normalise(2)
-        quant_xn(0)
-        copy_xn(1, 0, "s")
-        copy_xn(1, 1, "s")
-        normalise(3)
-        quant_xn(1)
-        copy_xn(2, 0, "s")
-        copy_xn(2, 1, "s")
-        copy_xn(3, 0, "v")
-        copy_xn(3, 1, "s")
-        quant_xn(2)
-        quant_xn(3)
-
         def regroup_x(g, eng):
             xg = xg_a if g < 2 else xg_b
             dst = xg[:, g % 2, :, :].rearrange("p (c i) t -> p c t i", i=4)
@@ -145,10 +129,35 @@ def tile_contranorm_pa_kernel(tc, x, out):
                 in_=xg[:].rearrange("p g d t -> p (g d t)"),
             )
 
+        sumsq(0)
+        sumsq(1)
+        normalise(0)
+        sumsq(2)
+        normalise(1)
+        sumsq(3)
+        copy_xn(0, 0, "s")
+        normalise(2)
+        copy_xn(0, 1, "s")
+        normalise(3)
+        quant_xn(0)
+        copy_xn(1, 0, "s")
+        copy_xn(1, 1, "s")
+        quant_xn(1)
+        copy_xn(2, 0, "s")
+        copy_xn(2, 1, "v")
+        copy_xn(3, 0, "s")
+        copy_xn(3, 1, "v")
+        quant_xn(2)
+        quant_xn(3)
+        nc.scalar.activation(out=dmy[:, 1:2], in_=one[:], func=ACT.Exp)
+        regroup_x(3, "s")
+        regroup_x(2, "s")
+
         s_t = {}
+        ssb_t = {}
         nm_t = {}
         e_t = {}
-        l4_t = {}
+        l_t = {}
         rl_t = {}
         tp_t = {}
         eg_t = {}
@@ -169,29 +178,30 @@ def tile_contranorm_pa_kernel(tc, x, out):
             s_t[(i, n)] = s
 
         def vmax(i):
+            s_sb = work.tile([P, N], F32, name="s_sb", tag="s_sb", bufs=3)
             mx4 = small.tile([P, 4], F32, name="mx4", tag="mx4")
             for n in range(4):
-                nc.vector.tensor_reduce(out=mx4[:, n : n + 1], in_=s_t[(i, n)][:], axis=AX.X, op=ALU.max)
+                nc.vector.tensor_scalar(
+                    out=s_sb[:, n * 512 : (n + 1) * 512], in0=s_t[(i, n)][:], scalar1=1.0, scalar2=None,
+                    op0=ALU.mult, op1=ALU.max, accum_out=mx4[:, n : n + 1],
+                )
             nm = small.tile([P, 1], F32, name="nm", tag="nm")
             nc.vector.tensor_reduce(out=nm[:], in_=mx4[:], axis=AX.X, op=ALU.max, negate=True)
             nm_t[i] = nm
+            ssb_t[i] = s_sb
 
         def expo(i):
-            e_sb = work.tile([P, N], BF16, name="e_sb", tag="e_sb")
-            l4 = small.tile([P, 4], F32, name="l4", tag="l4")
-            for n in range(4):
-                nc.scalar.activation(
-                    out=e_sb[:, n * 512 : (n + 1) * 512], in_=s_t[(i, n)][:], func=ACT.Exp,
-                    bias=nm_t[i][:, 0:1], scale=1.0, accum_out=l4[:, n : n + 1],
-                )
-            e_t[i] = e_sb
-            l4_t[i] = l4
-
-        def lsum(i):
+            e_sb = work.tile([P, N], BF16, name="e_sb", tag="e_sb", bufs=3)
             l1 = small.tile([P, 1], F32, name="l1", tag="l1")
-            nc.vector.tensor_reduce(out=l1[:], in_=l4_t[i][:], axis=AX.X, op=ALU.add)
+            nc.scalar.activation(
+                out=e_sb[:], in_=ssb_t[i][:], func=ACT.Exp, bias=nm_t[i][:, 0:1], scale=1.0, accum_out=l1[:, 0:1]
+            )
+            e_t[i] = e_sb
+            l_t[i] = l1
+
+        def lrec(i):
             rl = small.tile([P, 1], F32, name="rl", tag="rl")
-            nc.vector.reciprocal(out=rl[:], in_=l1[:])
+            nc.vector.reciprocal(out=rl[:], in_=l_t[i][:])
             rl_t[i] = rl
 
         def tr(i):
@@ -205,7 +215,7 @@ def tile_contranorm_pa_kernel(tc, x, out):
 
         def co(i, h, eng):
             if h == 0:
-                eg = work.tile([P, 4, P, 4], BF16, name="eg", tag="eg", align_bytes=64)
+                eg = work.tile([P, 4, P, 4], BF16, name="eg", tag="eg", bufs=3, align_bytes=64)
                 eg_t[i] = eg
             dst = eg_t[i][:, 2 * h : 2 * h + 2, :, :]
             src = tp_t[(i, h)][:].rearrange("p a t r -> p a r t")
@@ -215,8 +225,8 @@ def tile_contranorm_pa_kernel(tc, x, out):
                 nc.scalar.copy(out=dst, in_=src)
 
         def quant_e(i):
-            ec = work.tile([P, 512], U32, name="ec", tag="ec", align_bytes=64)
-            es = work.tile([P, 512], U8, name="es", tag="es", align_bytes=64)
+            ec = work.tile([P, 512], U32, name="ec", tag="ec", bufs=3, align_bytes=64)
+            es = work.tile([P, 512], U8, name="es", tag="es", bufs=3, align_bytes=64)
             nc.vector.quantize_mx(
                 out=ec[:].bitcast(FP8X4), scales=es[:], in_=eg_t[i][:].rearrange("p g r t -> p (g r t)")
             )
@@ -242,34 +252,24 @@ def tile_contranorm_pa_kernel(tc, x, out):
             nc.scalar.activation(out=o_sb[:], in_=o_t[i][:], func=ACT.Copy, scale=rl_t[i][:, 0:1])
             nc.sync.dma_start(out=out[i * P : (i + 1) * P, :], in_=o_sb[:])
 
-        nc.scalar.activation(out=dmy[:, 1:2], in_=one[:], func=ACT.Exp)
-        regroup_x(3, "s")
-
         for k in range(-1, NB + 2):
             has_a = 0 <= k + 1 < NB
             has_k = 0 <= k < NB
             has_c = 0 <= k - 1 < NB
             has_b = 0 <= k - 2 < NB
             if has_c:
-                lsum(k - 1)
-                co(k - 1, 0, "v")
+                lrec(k - 1)
+                co(k - 1, 0, "s" if ((k - 1) % 4 == 1 and k - 1 < 13) else "v")
             if has_k:
                 expo(k)
             if has_c:
-                co(k - 1, 1, "s")
+                co(k - 1, 1, "v" if k - 1 == 14 else "s")
             if has_a:
-                mm1(k + 1, 0)
+                for n in range(4):
+                    mm1(k + 1, n)
             if has_b:
-                mm2(k - 2, 0)
-                mm2(k - 2, 1)
-            if has_a:
-                mm1(k + 1, 1)
-            if has_b:
-                mm2(k - 2, 2)
-                mm2(k - 2, 3)
-            if has_a:
-                mm1(k + 1, 2)
-                mm1(k + 1, 3)
+                for g in range(4):
+                    mm2(k - 2, g)
             if k == -1:
                 regroup_x(0, "v")
             if k == 0:
@@ -277,7 +277,6 @@ def tile_contranorm_pa_kernel(tc, x, out):
             if has_a:
                 vmax(k + 1)
             if k == 0:
-                regroup_x(2, "v")
                 quant_x(0)
             if has_k:
                 tr(k)

@@ -16,7 +16,6 @@ P = 128
 N = 2048
 D = 512
 NB = N // P
-NCH = 4
 FLOPS = 2 * 2 * N * N * D
 
 
@@ -27,8 +26,8 @@ def tile_contranorm_pa_kernel(tc, x, out):
         work = ctx.enter_context(tc.tile_pool(name="work", bufs=2))
         small = ctx.enter_context(tc.tile_pool(name="small", bufs=6))
         ps_s = ctx.enter_context(tc.psum_pool(name="ps_s", bufs=4))
-        ps_t = ctx.enter_context(tc.psum_pool(name="ps_t", bufs=2))
-        ps_o = ctx.enter_context(tc.psum_pool(name="ps_o", bufs=2))
+        ps_t = ctx.enter_context(tc.psum_pool(name="ps_t", bufs=3))
+        ps_o = ctx.enter_context(tc.psum_pool(name="ps_o", bufs=1))
         ctx.enter_context(tc.manual_schedule())
 
         ident = const.tile([P, P], BF16, name="ident")
@@ -37,8 +36,8 @@ def tile_contranorm_pa_kernel(tc, x, out):
         xs = const.tile([P, N], U8, name="xs", align_bytes=64)
         xqc = const.tile([P, 4 * D], U32, name="xqc", align_bytes=64)
         xqs = const.tile([P, 4 * D], U8, name="xqs", align_bytes=64)
-        xg_a = const.tile([P, 2, D, 4], BF16, name="xg_a", align_bytes=64)
-        xg_b = const.tile([P, 2, D, 4], BF16, name="xg_b", align_bytes=64)
+        xg_2 = const.tile([P, D, 4], BF16, name="xg_2", align_bytes=64)
+        xg_3 = const.tile([P, D, 4], BF16, name="xg_3", align_bytes=64)
         ss_s = const.tile([P, 8], F32, name="ss_s")
         ss_v = const.tile([P, 8], F32, name="ss_v")
         ssc = const.tile([P, NB], F32, name="ssc")
@@ -48,8 +47,8 @@ def tile_contranorm_pa_kernel(tc, x, out):
         dmy = const.tile([P, 2], F32, name="dmy")
 
         x_v = x.rearrange("(c p) d -> p c d", p=P)
-        for c in range(NCH):
-            nc.sync.dma_start(out=x_sb[:, 4 * c : 4 * c + 4, :], in_=x_v[:, 4 * c : 4 * c + 4, :])
+        for b0, b1 in ((0, 1), (1, 2), (2, 4), (4, 8), (8, 12), (12, 16)):
+            nc.sync.dma_start(out=x_sb[:, b0:b1, :], in_=x_v[:, b0:b1, :])
 
         nc.vector.memset(one[:], 1.0)
         make_identity(nc, ident[:])
@@ -58,6 +57,7 @@ def tile_contranorm_pa_kernel(tc, x, out):
         xn_t = {}
         tx_t = {}
         xng_t = {}
+        xg_t = {2: xg_2, 3: xg_3}
 
         def sumsq(c):
             for a in range(2):
@@ -85,7 +85,7 @@ def tile_contranorm_pa_kernel(tc, x, out):
             for h in range(2):
                 if c < 2:
                     tx = ps_s.tile([P, 2, 4, P], BF16, name="tx", tag="s")
-                elif c == 2:
+                elif 2 * c + h < 7:
                     tx = ps_t.tile([P, 2, 4, P], BF16, name="tx", tag="t")
                 else:
                     tx = ps_o.tile([P, 2, 4, P], BF16, name="tx", tag="o")
@@ -96,7 +96,10 @@ def tile_contranorm_pa_kernel(tc, x, out):
 
         def copy_xn(c, h, eng):
             if h == 0:
-                xng = work.tile([P, 4, P, 4], BF16, name="xng", tag="xng", align_bytes=64)
+                if c < 3:
+                    xng = work.tile([P, 4, P, 4], BF16, name="xng", tag="xng", align_bytes=64)
+                else:
+                    xng = work.tile([P, 4, P, 4], BF16, name="xng", tag="xlast", bufs=1, align_bytes=64)
                 xng_t[c] = xng
             dst = xng_t[c][:, 2 * h : 2 * h + 2, :, :]
             src = tx_t[(c, h)][:].rearrange("p a t r -> p a r t")
@@ -112,49 +115,32 @@ def tile_contranorm_pa_kernel(tc, x, out):
                 in_=xng_t[c][:].rearrange("p a r t -> p (a r t)"),
             )
 
-        def regroup_x(g, eng):
-            xg = xg_a if g < 2 else xg_b
-            dst = xg[:, g % 2, :, :].rearrange("p (c i) t -> p c t i", i=4)
+        def regroup_x_scalar(g):
+            dst = xg_t[g][:].rearrange("p (c i) t -> p c t i", i=4)
             src = x_sb[:, 4 * g : 4 * g + 4, :].rearrange("p t (c i) -> p c t i", i=4)
-            if eng == "v":
-                nc.vector.tensor_copy(out=dst, in_=src)
-            else:
-                nc.scalar.copy(out=dst, in_=src)
+            nc.scalar.copy(out=dst, in_=src)
 
-        def quant_x(half):
-            xg = xg_a if half == 0 else xg_b
-            nc.vector.quantize_mx(
-                out=xqc[:, 1024 * half : 1024 * (half + 1)].bitcast(FP8X4),
-                scales=xqs[:, 1024 * half : 1024 * (half + 1)],
-                in_=xg[:].rearrange("p g d t -> p (g d t)"),
+        def regroup_x_gpsimd(g):
+            if g == 0:
+                xg = work.tile([P, D, 4], BF16, name="xg", tag="xlast", bufs=1, align_bytes=64)
+            else:
+                xg = work.tile([P, D, 4], BF16, name="xg", tag="xng", align_bytes=64)
+            xg_t[g] = xg
+            nc.gpsimd.tensor_scalar(
+                out=xg[:], in0=x_sb[:, 4 * g : 4 * g + 4, :].rearrange("p t d -> p d t"),
+                scalar1=1.0, scalar2=0.0, op0=ALU.mult, op1=ALU.add,
             )
 
-        sumsq(0)
-        sumsq(1)
-        normalise(0)
-        sumsq(2)
-        normalise(1)
-        sumsq(3)
-        copy_xn(0, 0, "s")
-        normalise(2)
-        copy_xn(0, 1, "s")
-        normalise(3)
-        quant_xn(0)
-        copy_xn(1, 0, "s")
-        copy_xn(1, 1, "s")
-        quant_xn(1)
-        copy_xn(2, 0, "s")
-        copy_xn(2, 1, "v")
-        copy_xn(3, 0, "s")
-        copy_xn(3, 1, "v")
-        quant_xn(2)
-        quant_xn(3)
-        nc.scalar.activation(out=dmy[:, 1:2], in_=one[:], func=ACT.Exp)
-        regroup_x(3, "s")
-        regroup_x(2, "s")
+        def quant_x(g):
+            nc.vector.quantize_mx(
+                out=xqc[:, D * g : D * (g + 1)].bitcast(FP8X4),
+                scales=xqs[:, D * g : D * (g + 1)],
+                in_=xg_t[g][:].rearrange("p d t -> p (d t)"),
+            )
 
         s_t = {}
         ssb_t = {}
+        mx_t = {}
         nm_t = {}
         e_t = {}
         l_t = {}
@@ -177,18 +163,26 @@ def tile_contranorm_pa_kernel(tc, x, out):
             )
             s_t[(i, n)] = s
 
-        def vmax(i):
-            s_sb = work.tile([P, N], F32, name="s_sb", tag="s_sb", bufs=3)
-            mx4 = small.tile([P, 4], F32, name="mx4", tag="mx4")
-            for n in range(4):
-                nc.vector.tensor_scalar(
-                    out=s_sb[:, n * 512 : (n + 1) * 512], in0=s_t[(i, n)][:], scalar1=1.0, scalar2=None,
-                    op0=ALU.mult, op1=ALU.max, accum_out=mx4[:, n : n + 1],
-                )
+        def vmaxc(i, n):
+            if n == 0:
+                s_sb = work.tile([P, N], F32, name="s_sb", tag="s_sb", bufs=3)
+                mx4 = small.tile([P, 4], F32, name="mx4", tag="mx4")
+                ssb_t[i] = s_sb
+                mx_t[i] = mx4
+            nc.vector.tensor_scalar(
+                out=ssb_t[i][:, n * 512 : (n + 1) * 512], in0=s_t[(i, n)][:], scalar1=1.0, scalar2=None,
+                op0=ALU.mult, op1=ALU.max, accum_out=mx_t[i][:, n : n + 1],
+            )
+
+        def vnm(i):
             nm = small.tile([P, 1], F32, name="nm", tag="nm")
-            nc.vector.tensor_reduce(out=nm[:], in_=mx4[:], axis=AX.X, op=ALU.max, negate=True)
+            nc.vector.tensor_reduce(out=nm[:], in_=mx_t[i][:], axis=AX.X, op=ALU.max, negate=True)
             nm_t[i] = nm
-            ssb_t[i] = s_sb
+
+        def vmax(i):
+            for n in range(4):
+                vmaxc(i, n)
+            vnm(i)
 
         def expo(i):
             e_sb = work.tile([P, N], BF16, name="e_sb", tag="e_sb", bufs=3)
@@ -199,25 +193,49 @@ def tile_contranorm_pa_kernel(tc, x, out):
             e_t[i] = e_sb
             l_t[i] = l1
 
+        def expo_halves(i):
+            e_sb = work.tile([P, N], BF16, name="e_sb", tag="e_sb", bufs=3)
+            l2 = small.tile([P, 2], F32, name="l2", tag="l2")
+            for h in range(2):
+                nc.scalar.activation(
+                    out=e_sb[:, h * 1024 : (h + 1) * 1024], in_=ssb_t[i][:, h * 1024 : (h + 1) * 1024], func=ACT.Exp,
+                    bias=nm_t[i][:, 0:1], scale=1.0, accum_out=l2[:, h : h + 1],
+                )
+            e_t[i] = e_sb
+            l_t[i] = l2
+
         def lrec(i):
             rl = small.tile([P, 1], F32, name="rl", tag="rl")
             nc.vector.reciprocal(out=rl[:], in_=l_t[i][:])
             rl_t[i] = rl
 
-        def tr(i):
-            for h in range(2):
-                tp = ps_t.tile([P, 2, 4, P], BF16, name="tp", tag="t")
-                for a in range(2):
-                    for t in range(4):
-                        j0 = (2 * h + a) * 512 + t * P
-                        nc.tensor.transpose(tp[:, a, t, :], e_t[i][:, j0 : j0 + P], ident[:])
-                tp_t[(i, h)] = tp
+        def lrec_halves(i):
+            l1 = small.tile([P, 1], F32, name="l1", tag="l1")
+            nc.vector.tensor_reduce(out=l1[:], in_=l_t[i][:], axis=AX.X, op=ALU.add)
+            rl = small.tile([P, 1], F32, name="rl", tag="rl")
+            nc.vector.reciprocal(out=rl[:], in_=l1[:])
+            rl_t[i] = rl
+
+        def tr(i, h):
+            tp = ps_t.tile([P, 2, 4, P], BF16, name="tp", tag="t")
+            for a in range(2):
+                for t in range(4):
+                    j0 = (2 * h + a) * 512 + t * P
+                    nc.tensor.transpose(tp[:, a, t, :], e_t[i][:, j0 : j0 + P], ident[:])
+            tp_t[(i, h)] = tp
 
         def co(i, h, eng):
             if h == 0:
                 eg = work.tile([P, 4, P, 4], BF16, name="eg", tag="eg", bufs=3, align_bytes=64)
                 eg_t[i] = eg
             dst = eg_t[i][:, 2 * h : 2 * h + 2, :, :]
+            if eng == "g":
+                et = work.tile([P, 2, 4, P], BF16, name="et", tag="et")
+                nc.vector.tensor_copy(out=et[:], in_=tp_t[(i, h)][:])
+                nc.gpsimd.tensor_scalar(
+                    out=dst, in0=et[:].rearrange("p a t r -> p a r t"), scalar1=1.0, scalar2=0.0, op0=ALU.mult, op1=ALU.add
+                )
+                return
             src = tp_t[(i, h)][:].rearrange("p a t r -> p a r t")
             if eng == "v":
                 nc.vector.tensor_copy(out=dst, in_=src)
@@ -231,6 +249,17 @@ def tile_contranorm_pa_kernel(tc, x, out):
                 out=ec[:].bitcast(FP8X4), scales=es[:], in_=eg_t[i][:].rearrange("p g r t -> p (g r t)")
             )
             ec_t[i] = (ec, es)
+
+        def quant_e_half(i, h):
+            if h == 0:
+                ec = work.tile([P, 512], U32, name="ec", tag="ec", bufs=3, align_bytes=64)
+                es = work.tile([P, 512], U8, name="es", tag="es", bufs=3, align_bytes=64)
+                ec_t[i] = (ec, es)
+            ec, es = ec_t[i]
+            nc.vector.quantize_mx(
+                out=ec[:, 256 * h : 256 * (h + 1)].bitcast(FP8X4), scales=es[:, 256 * h : 256 * (h + 1)],
+                in_=eg_t[i][:, 2 * h : 2 * h + 2, :, :].rearrange("p g r t -> p (g r t)"),
+            )
 
         def mm2(i, g):
             if g == 0:
@@ -252,37 +281,106 @@ def tile_contranorm_pa_kernel(tc, x, out):
             nc.scalar.activation(out=o_sb[:], in_=o_t[i][:], func=ACT.Copy, scale=rl_t[i][:, 0:1])
             nc.sync.dma_start(out=out[i * P : (i + 1) * P, :], in_=o_sb[:])
 
-        for k in range(-1, NB + 2):
-            has_a = 0 <= k + 1 < NB
-            has_k = 0 <= k < NB
-            has_c = 0 <= k - 1 < NB
-            has_b = 0 <= k - 2 < NB
-            if has_c:
+        sumsq(0)
+        sumsq(1)
+        normalise(0)
+        sumsq(2)
+        normalise(1)
+        sumsq(3)
+        copy_xn(0, 0, "s")
+        normalise(2)
+        copy_xn(0, 1, "s")
+        normalise(3)
+        quant_xn(0)
+        copy_xn(1, 0, "s")
+        copy_xn(1, 1, "s")
+        quant_xn(1)
+        copy_xn(2, 0, "s")
+        copy_xn(2, 1, "v")
+        mm1(0, 0)
+        mm1(0, 1)
+        quant_xn(2)
+        vmaxc(0, 0)
+        vmaxc(0, 1)
+        copy_xn(3, 0, "s")
+        copy_xn(3, 1, "v")
+        mm1(0, 2)
+        vmaxc(0, 2)
+        quant_xn(3)
+        mm1(0, 3)
+        vmaxc(0, 3)
+        vnm(0)
+        nc.scalar.activation(out=dmy[:, 1:2], in_=one[:], func=ACT.Exp)
+        regroup_x_scalar(3)
+        regroup_x_gpsimd(0)
+        regroup_x_gpsimd(1)
+
+        for k in range(0, NB - 1):
+            if k >= 1:
                 lrec(k - 1)
-                co(k - 1, 0, "s" if ((k - 1) % 4 == 1 and k - 1 < 13) else "v")
-            if has_k:
-                expo(k)
-            if has_c:
-                co(k - 1, 1, "v" if k - 1 == 14 else "s")
-            if has_a:
-                for n in range(4):
-                    mm1(k + 1, n)
-            if has_b:
+            if k >= 2:
+                quant_e(k - 2)
+                co(k - 1, 0, "g")
+            expo(k)
+            if k == 0:
+                regroup_x_scalar(2)
+            if k >= 1:
+                if k == 1:
+                    eg0 = work.tile([P, 4, P, 4], BF16, name="eg", tag="eg", bufs=3, align_bytes=64)
+                    eg_t[0] = eg0
+                co(k - 1, 1, "s")
+            for n in range(4):
+                mm1(k + 1, n)
+            if k >= 2:
                 for g in range(4):
                     mm2(k - 2, g)
-            if k == -1:
-                regroup_x(0, "v")
-            if k == 0:
-                regroup_x(1, "v")
-            if has_a:
-                vmax(k + 1)
-            if k == 0:
-                quant_x(0)
-            if has_k:
-                tr(k)
-            if has_c:
-                quant_e(k - 1)
+            vmax(k + 1)
             if k == 1:
-                quant_x(1)
-            if has_b:
+                for g in (3, 0, 2, 1):
+                    quant_x(g)
+                nc.vector.tensor_copy(out=eg_t[0][:, 0:2, :, :], in_=tp_t[(0, 0)][:].rearrange("p a t r -> p a r t"))
+            tr(k, 0)
+            tr(k, 1)
+            if k >= 2:
                 fin(k - 2)
+
+        last = NB - 1
+        lrec(last - 1)
+        quant_e(last - 2)
+        co(last - 1, 0, "v")
+        expo_halves(last)
+        co(last - 1, 1, "v")
+        for g in range(4):
+            mm2(last - 2, g)
+        tr(last, 0)
+        quant_e(last - 1)
+        tr(last, 1)
+        fin(last - 2)
+        for g in range(4):
+            mm2(last - 1, g)
+        co(last, 0, "v")
+        co(last, 1, "s")
+        lrec_halves(last)
+        quant_e_half(last, 0)
+        quant_e_half(last, 1)
+        o_a = ps_s.tile([P, 256], F32, name="o_a", tag="s")
+        o_b = ps_s.tile([P, 256], F32, name="o_b", tag="s")
+        ec, es = ec_t[last]
+        for g in range(4):
+            for o_half, c0 in ((o_a, 0), (o_b, 256)):
+                nc.tensor.matmul_mx(
+                    out=o_half[:],
+                    lhsT=ec[:, g * P : (g + 1) * P].bitcast(FP8X4),
+                    lhsT_scale=es[:, g * P : (g + 1) * P],
+                    rhs=xqc[:, g * D + c0 : g * D + c0 + 256].bitcast(FP8X4),
+                    rhs_scale=xqs[:, g * D + c0 : g * D + c0 + 256],
+                    start=(g == 0),
+                    stop=(g == 3),
+                )
+        fin(last - 1)
+        oa_sb = work.tile([P, 256], F32, name="oa_sb", tag="oa_sb", bufs=1)
+        ob_sb = work.tile([P, 256], F32, name="ob_sb", tag="ob_sb", bufs=1)
+        nc.vector.tensor_scalar_mul(out=oa_sb[:], in0=o_a[:], scalar1=rl_t[last][:, 0:1])
+        nc.scalar.activation(out=ob_sb[:], in_=o_b[:], func=ACT.Copy, scale=rl_t[last][:, 0:1])
+        nc.sync.dma_start(out=out[last * P : (last + 1) * P, 0:256], in_=oa_sb[:])
+        nc.scalar.dma_start(out=out[last * P : (last + 1) * P, 256:512], in_=ob_sb[:])

@@ -36,10 +36,9 @@ def tile_contranorm_pa_kernel(tc, x, out):
         xs = const.tile([P, N], U8, name="xs", align_bytes=64)
         xqc = const.tile([P, 4 * D], U32, name="xqc", align_bytes=64)
         xqs = const.tile([P, 4 * D], U8, name="xqs", align_bytes=64)
-        xg_2 = const.tile([P, D, 4], BF16, name="xg_2", align_bytes=64)
         xg_3 = const.tile([P, D, 4], BF16, name="xg_3", align_bytes=64)
-        ss_s = const.tile([P, 8], F32, name="ss_s")
-        ss_v = const.tile([P, 8], F32, name="ss_v")
+        ss_s = const.tile([P, NB], F32, name="ss_s")
+        ss_v = const.tile([P, NB], F32, name="ss_v")
         ssc = const.tile([P, NB], F32, name="ssc")
         nrm = const.tile([P, NB], F32, name="nrm")
         rn = const.tile([P, NB], F32, name="rn")
@@ -51,50 +50,60 @@ def tile_contranorm_pa_kernel(tc, x, out):
             nc.sync.dma_start(out=x_sb[:, b0:b1, :], in_=x_v[:, b0:b1, :])
 
         nc.vector.memset(one[:], 1.0)
+        nc.vector.memset(ss_s[:], 0.0)
+        nc.vector.memset(ss_v[:], 0.0)
         make_identity(nc, ident[:])
         nc.scalar.activation(out=dmy[:, 0:1], in_=one[:], func=ACT.Sqrt)
 
         xn_t = {}
         tx_t = {}
         xng_t = {}
-        xg_t = {2: xg_2, 3: xg_3}
+        xg_t = {3: xg_3}
 
-        def sumsq(c):
-            for a in range(2):
+        def sq(b, eng):
+            if eng == "s":
                 junk_s = work.tile([P, D], BF16, name="junk_s", tag="junk_s")
-                nc.scalar.activation(
-                    out=junk_s[:], in_=x_sb[:, 4 * c + a, :], func=ACT.Square,
-                    accum_out=ss_s[:, 2 * c + a : 2 * c + a + 1],
-                )
-            for a in range(2):
+                nc.scalar.activation(out=junk_s[:], in_=x_sb[:, b, :], func=ACT.Square, accum_out=ss_s[:, b : b + 1])
+            else:
                 junk_v = work.tile([P, D], F32, name="junk_v", tag="junk_v")
                 nc.vector.scalar_tensor_tensor(
-                    out=junk_v[:], in0=x_sb[:, 4 * c + 2 + a, :], scalar=1.0, in1=x_sb[:, 4 * c + 2 + a, :],
-                    op0=ALU.mult, op1=ALU.mult, accum_out=ss_v[:, 2 * c + a : 2 * c + a + 1],
+                    out=junk_v[:], in0=x_sb[:, b, :], scalar=1.0, in1=x_sb[:, b, :],
+                    op0=ALU.mult, op1=ALU.mult, accum_out=ss_v[:, b : b + 1],
                 )
-            nc.vector.tensor_scalar_max(out=ssc[:, 4 * c : 4 * c + 2], in0=ss_s[:, 2 * c : 2 * c + 2], scalar1=1e-24)
-            nc.vector.tensor_scalar_max(out=ssc[:, 4 * c + 2 : 4 * c + 4], in0=ss_v[:, 2 * c : 2 * c + 2], scalar1=1e-24)
 
-        def normalise(c):
+        def cl(c):
+            nc.vector.scalar_tensor_tensor(
+                out=ssc[:, 4 * c : 4 * c + 4], in0=ss_s[:, 4 * c : 4 * c + 4], scalar=1e-24, in1=ss_v[:, 4 * c : 4 * c + 4],
+                op0=ALU.max, op1=ALU.max,
+            )
+
+        def rt(c):
             nc.scalar.activation(out=nrm[:, 4 * c : 4 * c + 4], in_=ssc[:, 4 * c : 4 * c + 4], func=ACT.Sqrt)
+
+        def rc(c):
             nc.vector.reciprocal(out=rn[:, 4 * c : 4 * c + 4], in_=nrm[:, 4 * c : 4 * c + 4])
+
+        def xnorm(c):
             xn = work.tile([P, 4, D], BF16, name="xn", tag="xn", bufs=4)
             for a in range(4):
                 nc.vector.tensor_scalar_mul(out=xn[:, a, :], in0=x_sb[:, 4 * c + a, :], scalar1=rn[:, 4 * c + a : 4 * c + a + 1])
             xn_t[c] = xn
-            for h in range(2):
-                if c < 2:
-                    tx = ps_s.tile([P, 2, 4, P], BF16, name="tx", tag="s")
-                elif 2 * c + h < 7:
-                    tx = ps_t.tile([P, 2, 4, P], BF16, name="tx", tag="t")
-                else:
-                    tx = ps_o.tile([P, 2, 4, P], BF16, name="tx", tag="o")
-                for a in range(2):
-                    for t in range(4):
-                        nc.tensor.transpose(tx[:, a, t, :], xn[:, 2 * h + a, t * P : (t + 1) * P], ident[:])
-                tx_t[(c, h)] = tx
 
-        def copy_xn(c, h, eng):
+        def tx_bank(k):
+            if k < 4:
+                tx = ps_s.tile([P, 2, 4, P], BF16, name="tx", tag="s")
+            elif k < 7:
+                tx = ps_t.tile([P, 2, 4, P], BF16, name="tx", tag="t")
+            else:
+                tx = ps_o.tile([P, 2, 4, P], BF16, name="tx", tag="o")
+            for a in range(2):
+                for t in range(4):
+                    nc.tensor.transpose(tx[:, a, t, :], xn_t[k // 2][:, 2 * (k % 2) + a, t * P : (t + 1) * P], ident[:])
+            tx_t[k] = tx
+
+        def cox(k, eng):
+            c = k // 2
+            h = k % 2
             if h == 0:
                 if c < 3:
                     xng = work.tile([P, 4, P, 4], BF16, name="xng", tag="xng", align_bytes=64)
@@ -102,7 +111,7 @@ def tile_contranorm_pa_kernel(tc, x, out):
                     xng = work.tile([P, 4, P, 4], BF16, name="xng", tag="xlast", bufs=1, align_bytes=64)
                 xng_t[c] = xng
             dst = xng_t[c][:, 2 * h : 2 * h + 2, :, :]
-            src = tx_t[(c, h)][:].rearrange("p a t r -> p a r t")
+            src = tx_t[k][:].rearrange("p a t r -> p a r t")
             if eng == "v":
                 nc.vector.tensor_copy(out=dst, in_=src)
             else:
@@ -165,7 +174,7 @@ def tile_contranorm_pa_kernel(tc, x, out):
 
         def vmaxc(i, n):
             if n == 0:
-                s_sb = work.tile([P, N], F32, name="s_sb", tag="s_sb", bufs=3)
+                s_sb = work.tile([P, N], F32, name="s_sb", tag="s_sb", bufs=4)
                 mx4 = small.tile([P, 4], F32, name="mx4", tag="mx4")
                 ssb_t[i] = s_sb
                 mx_t[i] = mx4
@@ -276,73 +285,112 @@ def tile_contranorm_pa_kernel(tc, x, out):
                 stop=(g == 3),
             )
 
-        def fin(i):
+        def fin(i, eng):
             o_sb = work.tile([P, D], F32, name="o_sb", tag="o_sb", bufs=3)
-            nc.scalar.activation(out=o_sb[:], in_=o_t[i][:], func=ACT.Copy, scale=rl_t[i][:, 0:1])
+            if eng == "v":
+                nc.vector.tensor_scalar_mul(out=o_sb[:], in0=o_t[i][:], scalar1=rl_t[i][:, 0:1])
+            else:
+                nc.scalar.activation(out=o_sb[:], in_=o_t[i][:], func=ACT.Copy, scale=rl_t[i][:, 0:1])
             nc.sync.dma_start(out=out[i * P : (i + 1) * P, :], in_=o_sb[:])
 
-        sumsq(0)
-        sumsq(1)
-        normalise(0)
-        sumsq(2)
-        normalise(1)
-        sumsq(3)
-        copy_xn(0, 0, "s")
-        normalise(2)
-        copy_xn(0, 1, "s")
-        normalise(3)
+        sq(0, "s")
+        sq(1, "v")
+        sq(2, "s")
+        sq(3, "v")
+        cl(0)
+        rt(0)
+        sq(4, "v")
+        sq(5, "s")
+        rc(0)
+        sq(6, "s")
+        xnorm(0)
+        sq(7, "s")
+        sq(8, "v")
+        tx_bank(0)
+        sq(9, "s")
+        cl(1)
+        tx_bank(1)
+        sq(10, "v")
+        sq(11, "s")
+        sq(12, "v")
+        rt(1)
+        sq(13, "s")
+        rc(1)
+        cl(2)
+        sq(14, "s")
+        xnorm(1)
+        rt(2)
+        sq(15, "s")
+        rc(2)
+        xnorm(2)
+        tx_bank(2)
+        cox(0, "s")
+        tx_bank(3)
+        cl(3)
+        cox(1, "v")
+        tx_bank(4)
+        rt(3)
+        cox(2, "s")
+        tx_bank(5)
+        rc(3)
+        xnorm(3)
+        cox(3, "s")
         quant_xn(0)
-        copy_xn(1, 0, "s")
-        copy_xn(1, 1, "s")
-        quant_xn(1)
-        copy_xn(2, 0, "s")
-        copy_xn(2, 1, "v")
+        tx_bank(6)
+        cox(4, "s")
+        cox(5, "v")
+        tx_bank(7)
         mm1(0, 0)
-        mm1(0, 1)
+        cox(6, "s")
+        quant_xn(1)
         quant_xn(2)
+        mm1(0, 1)
+        cox(7, "s")
         vmaxc(0, 0)
-        vmaxc(0, 1)
-        copy_xn(3, 0, "s")
-        copy_xn(3, 1, "v")
         mm1(0, 2)
-        vmaxc(0, 2)
+        vmaxc(0, 1)
         quant_xn(3)
+        vmaxc(0, 2)
         mm1(0, 3)
         vmaxc(0, 3)
         vnm(0)
         nc.scalar.activation(out=dmy[:, 1:2], in_=one[:], func=ACT.Exp)
-        regroup_x_scalar(3)
         regroup_x_gpsimd(0)
         regroup_x_gpsimd(1)
+        regroup_x_gpsimd(2)
+        for n in range(4):
+            mm1(1, n)
+        vmax(1)
 
         for k in range(0, NB - 1):
+            late = k == NB - 2
             if k >= 1:
                 lrec(k - 1)
             if k >= 2:
                 quant_e(k - 2)
-                co(k - 1, 0, "g")
+                co(k - 1, 0, "v" if late else "g")
             expo(k)
             if k == 0:
-                regroup_x_scalar(2)
+                regroup_x_scalar(3)
+            if k == 1:
+                co(0, 0, "s")
             if k >= 1:
-                if k == 1:
-                    eg0 = work.tile([P, 4, P, 4], BF16, name="eg", tag="eg", bufs=3, align_bytes=64)
-                    eg_t[0] = eg0
-                co(k - 1, 1, "s")
-            for n in range(4):
-                mm1(k + 1, n)
+                co(k - 1, 1, "v" if late else "s")
+            if k + 2 < NB:
+                for n in range(4):
+                    mm1(k + 2, n)
             if k >= 2:
                 for g in range(4):
                     mm2(k - 2, g)
-            vmax(k + 1)
+            if k + 2 < NB:
+                vmax(k + 2)
             if k == 1:
-                for g in (3, 0, 2, 1):
+                for g in (3, 0, 1, 2):
                     quant_x(g)
-                nc.vector.tensor_copy(out=eg_t[0][:, 0:2, :, :], in_=tp_t[(0, 0)][:].rearrange("p a t r -> p a r t"))
             tr(k, 0)
             tr(k, 1)
             if k >= 2:
-                fin(k - 2)
+                fin(k - 2, "v" if late else "s")
 
         last = NB - 1
         lrec(last - 1)
@@ -355,7 +403,7 @@ def tile_contranorm_pa_kernel(tc, x, out):
         tr(last, 0)
         quant_e(last - 1)
         tr(last, 1)
-        fin(last - 2)
+        fin(last - 2, "s")
         for g in range(4):
             mm2(last - 1, g)
         co(last, 0, "v")
@@ -377,7 +425,7 @@ def tile_contranorm_pa_kernel(tc, x, out):
                     start=(g == 0),
                     stop=(g == 3),
                 )
-        fin(last - 1)
+        fin(last - 1, "s")
         oa_sb = work.tile([P, 256], F32, name="oa_sb", tag="oa_sb", bufs=1)
         ob_sb = work.tile([P, 256], F32, name="ob_sb", tag="ob_sb", bufs=1)
         nc.vector.tensor_scalar_mul(out=oa_sb[:], in0=o_a[:], scalar1=rl_t[last][:, 0:1])

@@ -361,6 +361,8 @@ def tile_contranorm_pa_kernel(tc, x, out):
         for n in range(4):
             mm1(1, n)
         vmax(1)
+        for n in range(4):
+            mm1(2, n)
 
         for k in range(0, NB - 1):
             late = k == NB - 2
@@ -376,9 +378,6 @@ def tile_contranorm_pa_kernel(tc, x, out):
                 co(0, 0, "s")
             if k >= 1:
                 co(k - 1, 1, "v" if late else "s")
-            if k + 2 < NB:
-                for n in range(4):
-                    mm1(k + 2, n)
             if k >= 2:
                 for g in range(4):
                     mm2(k - 2, g)
@@ -388,6 +387,9 @@ def tile_contranorm_pa_kernel(tc, x, out):
                 for g in (3, 0, 1, 2):
                     quant_x(g)
             tr(k, 0)
+            if k + 3 < NB:
+                for n in range(4):
+                    mm1(k + 3, n)
             tr(k, 1)
             if k >= 2:
                 fin(k - 2, "v" if late else "s")

@@ -30,7 +30,7 @@ def tile_contranorm_pa_kernel(tc, x, out):
         ps_o = ctx.enter_context(tc.psum_pool(name="ps_o", bufs=1))
         ctx.enter_context(tc.manual_schedule())
 
-        ident = const.tile([P, P], BF16, name="ident")
+        ident = const.tile([P, P], F32, name="ident")
         x_sb = const.tile([P, NB, D], BF16, name="x_sb")
         xc = const.tile([P, N], U32, name="xc", align_bytes=64)
         xs = const.tile([P, N], U8, name="xs", align_bytes=64)
@@ -45,9 +45,10 @@ def tile_contranorm_pa_kernel(tc, x, out):
         one = const.tile([P, 1], F32, name="one")
         dmy = const.tile([P, 2], F32, name="dmy")
 
-        x_v = x.rearrange("(c p) d -> p c d", p=P)
-        for b0, b1 in ((0, 1), (1, 2), (2, 4), (4, 8), (8, 12), (12, 16)):
-            nc.sync.dma_start(out=x_sb[:, b0:b1, :], in_=x_v[:, b0:b1, :])
+        x_v = x.rearrange("(u p e) d -> p u (e d)", p=P, e=2)
+        x_sv = x_sb[:].rearrange("p (u e) d -> p u (e d)", e=2)
+        for u0, u1 in ((0, 1), (1, 2), (2, 4), (4, 6), (6, 8)):
+            nc.sync.dma_start(out=x_sv[:, u0:u1, :], in_=x_v[:, u0:u1, :])
 
         nc.vector.memset(one[:], 1.0)
         nc.vector.memset(ss_s[:], 0.0)
@@ -91,14 +92,16 @@ def tile_contranorm_pa_kernel(tc, x, out):
 
         def tx_bank(k):
             if k < 4:
-                tx = ps_s.tile([P, 2, 4, P], BF16, name="tx", tag="s")
+                tx = ps_s.tile([P, 2, 2, P], F32, name="tx", tag="s")
             elif k < 7:
-                tx = ps_t.tile([P, 2, 4, P], BF16, name="tx", tag="t")
+                tx = ps_t.tile([P, 2, 2, P], F32, name="tx", tag="t")
             else:
-                tx = ps_o.tile([P, 2, 4, P], BF16, name="tx", tag="o")
-            for a in range(2):
-                for t in range(4):
-                    nc.tensor.transpose(tx[:, a, t, :], xn_t[k // 2][:, 2 * (k % 2) + a, t * P : (t + 1) * P], ident[:])
+                tx = ps_o.tile([P, 2, 2, P], F32, name="tx", tag="o")
+            words = xn_t[k // 2][:].rearrange("p a d -> p (a d)").bitcast(F32)
+            for e in range(2):
+                for v in range(2):
+                    w0 = (2 * (k % 2) + e) * 256 + v * P
+                    nc.tensor.transpose(tx[:, e, v, :], words[:, w0 : w0 + P], ident[:])
             tx_t[k] = tx
 
         def cox(k, eng):
@@ -106,12 +109,13 @@ def tile_contranorm_pa_kernel(tc, x, out):
             h = k % 2
             if h == 0:
                 if c < 3:
-                    xng = work.tile([P, 4, P, 4], BF16, name="xng", tag="xng", align_bytes=64)
+                    xng = work.tile([P, 512, 4], BF16, name="xng", tag="xng", align_bytes=64)
                 else:
-                    xng = work.tile([P, 4, P, 4], BF16, name="xng", tag="xlast", bufs=1, align_bytes=64)
+                    xng = work.tile([P, 512, 4], BF16, name="xng", tag="xlast", bufs=1, align_bytes=64)
                 xng_t[c] = xng
-            dst = xng_t[c][:, 2 * h : 2 * h + 2, :, :]
-            src = tx_t[k][:].rearrange("p a t r -> p a r t")
+            words = xng_t[c][:].rearrange("p c t -> p (c t)").bitcast(F32)
+            dst = words[:, 512 * h : 512 * (h + 1)].rearrange("p (r e v) -> p r e v", e=2, v=2)
+            src = tx_t[k][:].rearrange("p e v r -> p r e v")
             if eng == "v":
                 nc.vector.tensor_copy(out=dst, in_=src)
             else:
@@ -121,7 +125,7 @@ def tile_contranorm_pa_kernel(tc, x, out):
             nc.vector.quantize_mx(
                 out=xc[:, 512 * c : 512 * (c + 1)].bitcast(FP8X4),
                 scales=xs[:, 512 * c : 512 * (c + 1)],
-                in_=xng_t[c][:].rearrange("p a r t -> p (a r t)"),
+                in_=xng_t[c][:].rearrange("p c t -> p (c t)"),
             )
 
         def regroup_x_scalar(g):
@@ -226,26 +230,20 @@ def tile_contranorm_pa_kernel(tc, x, out):
             rl_t[i] = rl
 
         def tr(i, h):
-            tp = ps_t.tile([P, 2, 4, P], BF16, name="tp", tag="t")
-            for a in range(2):
-                for t in range(4):
-                    j0 = (2 * h + a) * 512 + t * P
-                    nc.tensor.transpose(tp[:, a, t, :], e_t[i][:, j0 : j0 + P], ident[:])
+            tp = ps_t.tile([P, 4, P], F32, name="tp", tag="t")
+            words = e_t[i][:].bitcast(F32)
+            for q in range(4):
+                w0 = (4 * h + q) * P
+                nc.tensor.transpose(tp[:, q, :], words[:, w0 : w0 + P], ident[:])
             tp_t[(i, h)] = tp
 
         def co(i, h, eng):
             if h == 0:
                 eg = work.tile([P, 4, P, 4], BF16, name="eg", tag="eg", bufs=3, align_bytes=64)
                 eg_t[i] = eg
-            dst = eg_t[i][:, 2 * h : 2 * h + 2, :, :]
-            if eng == "g":
-                et = work.tile([P, 2, 4, P], BF16, name="et", tag="et")
-                nc.vector.tensor_copy(out=et[:], in_=tp_t[(i, h)][:])
-                nc.gpsimd.tensor_scalar(
-                    out=dst, in0=et[:].rearrange("p a t r -> p a r t"), scalar1=1.0, scalar2=0.0, op0=ALU.mult, op1=ALU.add
-                )
-                return
-            src = tp_t[(i, h)][:].rearrange("p a t r -> p a r t")
+            words = eg_t[i][:].rearrange("p g r t -> p (g r t)").bitcast(F32)
+            dst = words[:, 512 * h : 512 * (h + 1)].rearrange("p (g r v) -> p g r v", g=2, v=2)
+            src = tp_t[(i, h)][:].rearrange("p (g v) r -> p g r v", v=2)
             if eng == "v":
                 nc.vector.tensor_copy(out=dst, in_=src)
             else:
@@ -370,7 +368,7 @@ def tile_contranorm_pa_kernel(tc, x, out):
                 lrec(k - 1)
             if k >= 2:
                 quant_e(k - 2)
-                co(k - 1, 0, "v" if late else "g")
+                co(k - 1, 0, "v")
             expo(k)
             if k == 0:
                 regroup_x_scalar(3)

@@ -24,7 +24,7 @@ def tile_contranorm_pa_kernel(tc, x, out):
     with ExitStack() as ctx:
         const = ctx.enter_context(tc.tile_pool(name="const", bufs=1))
         work = ctx.enter_context(tc.tile_pool(name="work", bufs=2))
-        small = ctx.enter_context(tc.tile_pool(name="small", bufs=6))
+        small = ctx.enter_context(tc.tile_pool(name="small", bufs=8))
         ps_s = ctx.enter_context(tc.psum_pool(name="ps_s", bufs=4))
         ps_t = ctx.enter_context(tc.psum_pool(name="ps_t", bufs=3))
         ps_o = ctx.enter_context(tc.psum_pool(name="ps_o", bufs=1))
@@ -37,24 +37,22 @@ def tile_contranorm_pa_kernel(tc, x, out):
         xqc = const.tile([P, 4 * D], U32, name="xqc", align_bytes=64)
         xqs = const.tile([P, 4 * D], U8, name="xqs", align_bytes=64)
         xg_3 = const.tile([P, D, 4], BF16, name="xg_3", align_bytes=64)
-        ss_s = const.tile([P, NB], F32, name="ss_s")
-        ss_v = const.tile([P, NB], F32, name="ss_v")
+        ss = const.tile([P, NB], F32, name="ss")
         ssc = const.tile([P, NB], F32, name="ssc")
-        nrm = const.tile([P, NB], F32, name="nrm")
+        mhalf = const.tile([P, NB], F32, name="mhalf")
         rn = const.tile([P, NB], F32, name="rn")
         one = const.tile([P, 1], F32, name="one")
-        dmy = const.tile([P, 2], F32, name="dmy")
+        dmy = const.tile([P, 1], F32, name="dmy")
 
         x_v = x.rearrange("(u p e) d -> p u (e d)", p=P, e=2)
         x_sv = x_sb[:].rearrange("p (u e) d -> p u (e d)", e=2)
-        for u0, u1 in ((0, 1), (1, 2), (2, 4), (4, 6), (6, 8)):
+        for u0, u1 in ((0, 1), (1, 2), (2, 3), (3, 4), (4, 6), (6, 8)):
             nc.sync.dma_start(out=x_sv[:, u0:u1, :], in_=x_v[:, u0:u1, :])
 
         nc.vector.memset(one[:], 1.0)
-        nc.vector.memset(ss_s[:], 0.0)
-        nc.vector.memset(ss_v[:], 0.0)
+        nc.gpsimd.memset(mhalf[:], -0.5)
         make_identity(nc, ident[:])
-        nc.scalar.activation(out=dmy[:, 0:1], in_=one[:], func=ACT.Sqrt)
+        nc.scalar.activation(out=dmy[:], in_=one[:], func=ACT.Exp)
 
         xn_t = {}
         tx_t = {}
@@ -64,31 +62,25 @@ def tile_contranorm_pa_kernel(tc, x, out):
         def sq(b, eng):
             if eng == "s":
                 junk_s = work.tile([P, D], BF16, name="junk_s", tag="junk_s")
-                nc.scalar.activation(out=junk_s[:], in_=x_sb[:, b, :], func=ACT.Square, accum_out=ss_s[:, b : b + 1])
+                nc.scalar.activation(out=junk_s[:], in_=x_sb[:, b, :], func=ACT.Square, accum_out=ss[:, b : b + 1])
             else:
                 junk_v = work.tile([P, D], F32, name="junk_v", tag="junk_v")
                 nc.vector.scalar_tensor_tensor(
                     out=junk_v[:], in0=x_sb[:, b, :], scalar=1.0, in1=x_sb[:, b, :],
-                    op0=ALU.mult, op1=ALU.mult, accum_out=ss_v[:, b : b + 1],
+                    op0=ALU.mult, op1=ALU.mult, accum_out=ss[:, b : b + 1],
                 )
 
-        def cl(c):
-            nc.vector.scalar_tensor_tensor(
-                out=ssc[:, 4 * c : 4 * c + 4], in0=ss_s[:, 4 * c : 4 * c + 4], scalar=1e-24, in1=ss_v[:, 4 * c : 4 * c + 4],
-                op0=ALU.max, op1=ALU.max,
-            )
+        def inv(u):
+            cols = slice(2 * u, 2 * u + 2)
+            nc.gpsimd.tensor_scalar(out=ssc[:, cols], in0=ss[:, cols], scalar1=1e-24, scalar2=None, op0=ALU.max)
+            nc.gpsimd.tensor_tensor(out=rn[:, cols], in0=ssc[:, cols], in1=mhalf[:, cols], op=ALU.pow)
 
-        def rt(c):
-            nc.scalar.activation(out=nrm[:, 4 * c : 4 * c + 4], in_=ssc[:, 4 * c : 4 * c + 4], func=ACT.Sqrt)
-
-        def rc(c):
-            nc.vector.reciprocal(out=rn[:, 4 * c : 4 * c + 4], in_=nrm[:, 4 * c : 4 * c + 4])
-
-        def xnorm(c):
-            xn = work.tile([P, 4, D], BF16, name="xn", tag="xn", bufs=4)
-            for a in range(4):
-                nc.vector.tensor_scalar_mul(out=xn[:, a, :], in0=x_sb[:, 4 * c + a, :], scalar1=rn[:, 4 * c + a : 4 * c + a + 1])
-            xn_t[c] = xn
+        def xnorm(u):
+            xn = work.tile([P, 2, D], BF16, name="xn", tag="xn", bufs=8)
+            for e in range(2):
+                b = 2 * u + e
+                nc.vector.tensor_scalar_mul(out=xn[:, e, :], in0=x_sb[:, b, :], scalar1=rn[:, b : b + 1])
+            xn_t[u] = xn
 
         def tx_bank(k):
             if k < 4:
@@ -97,10 +89,10 @@ def tile_contranorm_pa_kernel(tc, x, out):
                 tx = ps_t.tile([P, 2, 2, P], F32, name="tx", tag="t")
             else:
                 tx = ps_o.tile([P, 2, 2, P], F32, name="tx", tag="o")
-            words = xn_t[k // 2][:].rearrange("p a d -> p (a d)").bitcast(F32)
+            words = xn_t[k][:].rearrange("p a d -> p (a d)").bitcast(F32)
             for e in range(2):
                 for v in range(2):
-                    w0 = (2 * (k % 2) + e) * 256 + v * P
+                    w0 = e * 256 + v * P
                     nc.tensor.transpose(tx[:, e, v, :], words[:, w0 : w0 + P], ident[:])
             tx_t[k] = tx
 
@@ -120,6 +112,13 @@ def tile_contranorm_pa_kernel(tc, x, out):
                 nc.vector.tensor_copy(out=dst, in_=src)
             else:
                 nc.scalar.copy(out=dst, in_=src)
+
+        def quant_xn_half(c, h):
+            nc.vector.quantize_mx(
+                out=xc[:, 512 * c + 256 * h : 512 * c + 256 * (h + 1)].bitcast(FP8X4),
+                scales=xs[:, 512 * c + 256 * h : 512 * c + 256 * (h + 1)],
+                in_=xng_t[c][:, 256 * h : 256 * (h + 1), :].rearrange("p c t -> p (c t)"),
+            )
 
         def quant_xn(c):
             nc.vector.quantize_mx(
@@ -198,7 +197,7 @@ def tile_contranorm_pa_kernel(tc, x, out):
             vnm(i)
 
         def expo(i):
-            e_sb = work.tile([P, N], BF16, name="e_sb", tag="e_sb", bufs=3)
+            e_sb = work.tile([P, N], BF16, name="e_sb", tag="e_sb", bufs=4)
             l1 = small.tile([P, 1], F32, name="l1", tag="l1")
             nc.scalar.activation(
                 out=e_sb[:], in_=ssb_t[i][:], func=ACT.Exp, bias=nm_t[i][:, 0:1], scale=1.0, accum_out=l1[:, 0:1]
@@ -207,7 +206,7 @@ def tile_contranorm_pa_kernel(tc, x, out):
             l_t[i] = l1
 
         def expo_halves(i):
-            e_sb = work.tile([P, N], BF16, name="e_sb", tag="e_sb", bufs=3)
+            e_sb = work.tile([P, N], BF16, name="e_sb", tag="e_sb", bufs=4)
             l2 = small.tile([P, 2], F32, name="l2", tag="l2")
             for h in range(2):
                 nc.scalar.activation(
@@ -239,7 +238,7 @@ def tile_contranorm_pa_kernel(tc, x, out):
 
         def co(i, h, eng):
             if h == 0:
-                eg = work.tile([P, 4, P, 4], BF16, name="eg", tag="eg", bufs=3, align_bytes=64)
+                eg = work.tile([P, 4, P, 4], BF16, name="eg", tag="eg", bufs=4, align_bytes=64)
                 eg_t[i] = eg
             words = eg_t[i][:].rearrange("p g r t -> p (g r t)").bitcast(F32)
             dst = words[:, 512 * h : 512 * (h + 1)].rearrange("p (g r v) -> p g r v", g=2, v=2)
@@ -250,8 +249,8 @@ def tile_contranorm_pa_kernel(tc, x, out):
                 nc.scalar.copy(out=dst, in_=src)
 
         def quant_e(i):
-            ec = work.tile([P, 512], U32, name="ec", tag="ec", bufs=3, align_bytes=64)
-            es = work.tile([P, 512], U8, name="es", tag="es", bufs=3, align_bytes=64)
+            ec = work.tile([P, 512], U32, name="ec", tag="ec", bufs=4, align_bytes=64)
+            es = work.tile([P, 512], U8, name="es", tag="es", bufs=4, align_bytes=64)
             nc.vector.quantize_mx(
                 out=ec[:].bitcast(FP8X4), scales=es[:], in_=eg_t[i][:].rearrange("p g r t -> p (g r t)")
             )
@@ -259,8 +258,8 @@ def tile_contranorm_pa_kernel(tc, x, out):
 
         def quant_e_half(i, h):
             if h == 0:
-                ec = work.tile([P, 512], U32, name="ec", tag="ec", bufs=3, align_bytes=64)
-                es = work.tile([P, 512], U8, name="es", tag="es", bufs=3, align_bytes=64)
+                ec = work.tile([P, 512], U32, name="ec", tag="ec", bufs=4, align_bytes=64)
+                es = work.tile([P, 512], U8, name="es", tag="es", bufs=4, align_bytes=64)
                 ec_t[i] = (ec, es)
             ec, es = ec_t[i]
             nc.vector.quantize_mx(
@@ -270,7 +269,10 @@ def tile_contranorm_pa_kernel(tc, x, out):
 
         def mm2(i, g):
             if g == 0:
-                o_ps = ps_o.tile([P, D], F32, name="o_ps", tag="o")
+                if i < NB - 4:
+                    o_ps = ps_o.tile([P, D], F32, name="o_ps", tag="o")
+                else:
+                    o_ps = ps_s.tile([P, D], F32, name="o_ps", tag="s")
                 o_t[i] = o_ps
             ec, es = ec_t[i]
             nc.tensor.matmul_mx(
@@ -284,75 +286,42 @@ def tile_contranorm_pa_kernel(tc, x, out):
             )
 
         def fin(i, eng):
-            o_sb = work.tile([P, D], F32, name="o_sb", tag="o_sb", bufs=3)
+            o_sb = work.tile([P, D], F32, name="o_sb", tag="o_sb", bufs=4)
             if eng == "v":
                 nc.vector.tensor_scalar_mul(out=o_sb[:], in0=o_t[i][:], scalar1=rl_t[i][:, 0:1])
             else:
                 nc.scalar.activation(out=o_sb[:], in_=o_t[i][:], func=ACT.Copy, scale=rl_t[i][:, 0:1])
             nc.sync.dma_start(out=out[i * P : (i + 1) * P, :], in_=o_sb[:])
 
-        sq(0, "s")
-        sq(1, "v")
-        sq(2, "s")
-        sq(3, "v")
-        cl(0)
-        rt(0)
-        sq(4, "v")
-        sq(5, "s")
-        rc(0)
-        sq(6, "s")
-        xnorm(0)
-        sq(7, "s")
-        sq(8, "v")
-        tx_bank(0)
-        sq(9, "s")
-        cl(1)
-        tx_bank(1)
-        sq(10, "v")
-        sq(11, "s")
-        sq(12, "v")
-        rt(1)
-        sq(13, "s")
-        rc(1)
-        cl(2)
-        sq(14, "s")
-        xnorm(1)
-        rt(2)
-        sq(15, "s")
-        rc(2)
-        xnorm(2)
-        tx_bank(2)
-        cox(0, "s")
-        tx_bank(3)
-        cl(3)
-        cox(1, "v")
-        tx_bank(4)
-        rt(3)
-        cox(2, "s")
-        tx_bank(5)
-        rc(3)
-        xnorm(3)
-        cox(3, "s")
-        quant_xn(0)
-        tx_bank(6)
-        cox(4, "s")
-        cox(5, "v")
-        tx_bank(7)
+        squares_on_vector = (1, 3, 5)
+        for b in range(6):
+            sq(b, "v" if b in squares_on_vector else "s")
+            if b % 2:
+                inv(b // 2)
+        for u in range(8):
+            if u + 3 < 8:
+                for b in (2 * u + 6, 2 * u + 7):
+                    sq(b, "v" if b in squares_on_vector else "s")
+                inv(u + 3)
+            xnorm(u)
+            tx_bank(u)
+            if u >= 1:
+                cox(u - 1, "v" if u <= 5 else "s")
+            if u in (3, 5):
+                quant_xn((u - 3) // 2)
         mm1(0, 0)
-        cox(6, "s")
-        quant_xn(1)
-        quant_xn(2)
         mm1(0, 1)
-        cox(7, "s")
+        quant_xn(2)
         vmaxc(0, 0)
-        mm1(0, 2)
         vmaxc(0, 1)
+        mm1(0, 2)
+        cox(7, "s")
         quant_xn(3)
         vmaxc(0, 2)
         mm1(0, 3)
         vmaxc(0, 3)
         vnm(0)
-        nc.scalar.activation(out=dmy[:, 1:2], in_=one[:], func=ACT.Exp)
+        regroup_x_scalar(3)
         regroup_x_gpsimd(0)
         regroup_x_gpsimd(1)
         regroup_x_gpsimd(2)
@@ -362,56 +331,68 @@ def tile_contranorm_pa_kernel(tc, x, out):
         for n in range(4):
             mm1(2, n)
 
-        for k in range(0, NB - 1):
-            late = k == NB - 2
-            if k >= 1:
-                lrec(k - 1)
+        for k in range(NB - 2):
+            expo(k)
+            if k >= 3:
+                for g in range(4):
+                    mm2(k - 3, g)
+            for n in range(4):
+                vmaxc(k + 2, n)
             if k >= 2:
                 quant_e(k - 2)
-                co(k - 1, 0, "v")
-            expo(k)
-            if k == 0:
-                regroup_x_scalar(3)
-            if k == 1:
-                co(0, 0, "s")
-            if k >= 1:
-                co(k - 1, 1, "v" if late else "s")
-            if k >= 2:
-                for g in range(4):
-                    mm2(k - 2, g)
-            if k + 2 < NB:
-                vmax(k + 2)
+            vnm(k + 2)
             if k == 1:
                 for g in (3, 0, 1, 2):
                     quant_x(g)
-            tr(k, 0)
+            if k >= 1:
+                lrec(k - 1)
+                co(k - 1, 0, "s")
+                co(k - 1, 1, "s")
+            if k >= 3:
+                fin(k - 3, "s" if k < 8 else "v")
+            if k <= 2:
+                tr(k, 0)
+                tr(k, 1)
             if k + 3 < NB:
                 for n in range(4):
                     mm1(k + 3, n)
-            tr(k, 1)
-            if k >= 2:
-                fin(k - 2, "v" if late else "s")
+            if not (k <= 2):
+                tr(k, 0)
+                tr(k, 1)
 
+        expo(14)
+        for g in range(4):
+            mm2(11, g)
+        quant_e(12)
+        co(13, 0, "v")
+        lrec(13)
+        co(13, 1, "v")
+        tr(14, 0)
+        tr(14, 1)
+        expo_halves(15)
+        fin(11, "v")
+        quant_e(13)
+        for g in range(4):
+            mm2(12, g)
+        co(14, 0, "v")
+        lrec(14)
+        co(14, 1, "s")
+        tr(15, 0)
+        tr(15, 1)
+        for g in range(4):
+            mm2(13, g)
+        co(15, 0, "v")
+        quant_e(14)
+        co(15, 1, "s")
+        quant_e_half(15, 0)
+        lrec_halves(15)
+        fin(12, "s")
+        for g in range(4):
+            mm2(14, g)
+        quant_e_half(15, 1)
+        fin(13, "v")
         last = NB - 1
-        lrec(last - 1)
-        quant_e(last - 2)
-        co(last - 1, 0, "v")
-        expo_halves(last)
-        co(last - 1, 1, "v")
-        for g in range(4):
-            mm2(last - 2, g)
-        tr(last, 0)
-        quant_e(last - 1)
-        tr(last, 1)
-        fin(last - 2, "s")
-        for g in range(4):
-            mm2(last - 1, g)
-        co(last, 0, "v")
-        co(last, 1, "s")
-        lrec_halves(last)
-        quant_e_half(last, 0)
-        quant_e_half(last, 1)
-        o_a = ps_s.tile([P, 256], F32, name="o_a", tag="s")
+        o_a = ps_o.tile([P, 256], F32, name="o_a", tag="o")
         o_b = ps_s.tile([P, 256], F32, name="o_b", tag="s")
         ec, es = ec_t[last]
         for g in range(4):

@@ -39,10 +39,10 @@ def tile_contranorm_pa_kernel(tc, x, out):
         xg_3 = const.tile([P, D, 4], BF16, name="xg_3", align_bytes=64)
         ss = const.tile([P, NB], F32, name="ss")
         ssc = const.tile([P, NB], F32, name="ssc")
-        mhalf = const.tile([P, NB], F32, name="mhalf")
+        nrm = const.tile([P, NB], F32, name="nrm")
         rn = const.tile([P, NB], F32, name="rn")
         one = const.tile([P, 1], F32, name="one")
-        dmy = const.tile([P, 1], F32, name="dmy")
+        dmy = const.tile([P, 2], F32, name="dmy")
 
         x_v = x.rearrange("(u p e) d -> p u (e d)", p=P, e=2)
         x_sv = x_sb[:].rearrange("p (u e) d -> p u (e d)", e=2)
@@ -50,9 +50,8 @@ def tile_contranorm_pa_kernel(tc, x, out):
             nc.sync.dma_start(out=x_sv[:, u0:u1, :], in_=x_v[:, u0:u1, :])
 
         nc.vector.memset(one[:], 1.0)
-        nc.gpsimd.memset(mhalf[:], -0.5)
         make_identity(nc, ident[:])
-        nc.scalar.activation(out=dmy[:], in_=one[:], func=ACT.Exp)
+        nc.scalar.activation(out=dmy[:, 0:1], in_=one[:], func=ACT.Sqrt)
 
         xn_t = {}
         tx_t = {}
@@ -70,10 +69,17 @@ def tile_contranorm_pa_kernel(tc, x, out):
                     op0=ALU.mult, op1=ALU.mult, accum_out=ss[:, b : b + 1],
                 )
 
-        def inv(u):
-            cols = slice(2 * u, 2 * u + 2)
-            nc.gpsimd.tensor_scalar(out=ssc[:, cols], in0=ss[:, cols], scalar1=1e-24, scalar2=None, op0=ALU.max)
-            nc.gpsimd.tensor_tensor(out=rn[:, cols], in0=ssc[:, cols], in1=mhalf[:, cols], op=ALU.pow)
+        def cl(c):
+            cols = slice(4 * c, 4 * c + 4)
+            nc.vector.tensor_scalar_max(out=ssc[:, cols], in0=ss[:, cols], scalar1=1e-24)
+
+        def rt(c):
+            cols = slice(4 * c, 4 * c + 4)
+            nc.scalar.activation(out=nrm[:, cols], in_=ssc[:, cols], func=ACT.Sqrt)
+
+        def rc(c):
+            cols = slice(4 * c, 4 * c + 4)
+            nc.vector.reciprocal(out=rn[:, cols], in_=nrm[:, cols])
 
         def xnorm(u):
             xn = work.tile([P, 2, D], BF16, name="xn", tag="xn", bufs=8)
@@ -293,24 +299,57 @@ def tile_contranorm_pa_kernel(tc, x, out):
                 nc.scalar.activation(out=o_sb[:], in_=o_t[i][:], func=ACT.Copy, scale=rl_t[i][:, 0:1])
             nc.sync.dma_start(out=out[i * P : (i + 1) * P, :], in_=o_sb[:])
 
-        squares_on_vector = (1, 3, 5)
-        for b in range(6):
-            sq(b, "v" if b in squares_on_vector else "s")
-            if b % 2:
-                inv(b // 2)
-        for u in range(8):
-            if u + 3 < 8:
-                for b in (2 * u + 6, 2 * u + 7):
-                    sq(b, "v" if b in squares_on_vector else "s")
-                inv(u + 3)
-            xnorm(u)
-            tx_bank(u)
-            if u >= 1:
-                cox(u - 1, "v" if u <= 5 else "s")
-            if u in (3, 5):
-                quant_xn((u - 3) // 2)
+        squares_on_vector = (1, 3, 7)
+
+        def sqs(b0, b1):
+            for b in range(b0, b1):
+                sq(b, "v" if b in squares_on_vector else "s")
+
+        sqs(0, 5)
+        cl(0)
+        rt(0)
+        sqs(5, 8)
+        rc(0)
+        xnorm(0)
+        tx_bank(0)
+        xnorm(1)
+        tx_bank(1)
+        cl(1)
+        sqs(8, 9)
+        rt(1)
+        cox(0, "v")
+        sqs(9, 12)
+        rc(1)
+        cox(1, "v")
+        xnorm(2)
+        tx_bank(2)
+        xnorm(3)
+        tx_bank(3)
+        cl(2)
+        sqs(12, 13)
+        rt(2)
+        quant_xn(0)
+        sqs(13, 16)
+        rc(2)
+        cox(2, "v")
+        xnorm(4)
+        tx_bank(4)
+        xnorm(5)
+        tx_bank(5)
+        cox(3, "v")
+        cl(3)
+        rt(3)
+        quant_xn(1)
+        rc(3)
+        cox(4, "s")
+        xnorm(6)
+        tx_bank(6)
+        xnorm(7)
+        tx_bank(7)
         mm1(0, 0)
         mm1(0, 1)
+        cox(5, "s")
+        cox(6, "s")
         quant_xn(2)
         vmaxc(0, 0)
         vmaxc(0, 1)
@@ -321,6 +360,7 @@ def tile_contranorm_pa_kernel(tc, x, out):
         mm1(0, 3)
         vmaxc(0, 3)
         vnm(0)
+        nc.scalar.activation(out=dmy[:, 1:2], in_=one[:], func=ACT.Exp)
         regroup_x_scalar(3)
         regroup_x_gpsimd(0)
         regroup_x_gpsimd(1)

@@ -26,8 +26,8 @@ def tile_contranorm_pa_kernel(tc, x, out):
         work = ctx.enter_context(tc.tile_pool(name="work", bufs=2))
         small = ctx.enter_context(tc.tile_pool(name="small", bufs=8))
         ps_s = ctx.enter_context(tc.psum_pool(name="ps_s", bufs=4))
-        ps_t = ctx.enter_context(tc.psum_pool(name="ps_t", bufs=3))
-        ps_o = ctx.enter_context(tc.psum_pool(name="ps_o", bufs=1))
+        ps_t = ctx.enter_context(tc.psum_pool(name="ps_t", bufs=2))
+        ps_o = ctx.enter_context(tc.psum_pool(name="ps_o", bufs=2))
         ctx.enter_context(tc.manual_schedule())
 
         ident = const.tile([P, P], F32, name="ident")
@@ -91,7 +91,7 @@ def tile_contranorm_pa_kernel(tc, x, out):
         def tx_bank(k):
             if k < 4:
                 tx = ps_s.tile([P, 2, 2, P], F32, name="tx", tag="s")
-            elif k < 7:
+            elif k < 6:
                 tx = ps_t.tile([P, 2, 2, P], F32, name="tx", tag="t")
             else:
                 tx = ps_o.tile([P, 2, 2, P], F32, name="tx", tag="o")
@@ -211,48 +211,58 @@ def tile_contranorm_pa_kernel(tc, x, out):
             e_t[i] = e_sb
             l_t[i] = l1
 
-        def expo_halves(i):
-            e_sb = work.tile([P, N], BF16, name="e_sb", tag="e_sb", bufs=4)
-            l2 = small.tile([P, 2], F32, name="l2", tag="l2")
-            for h in range(2):
-                nc.scalar.activation(
-                    out=e_sb[:, h * 1024 : (h + 1) * 1024], in_=ssb_t[i][:, h * 1024 : (h + 1) * 1024], func=ACT.Exp,
-                    bias=nm_t[i][:, 0:1], scale=1.0, accum_out=l2[:, h : h + 1],
-                )
-            e_t[i] = e_sb
-            l_t[i] = l2
+        def expo_piece(i, c0, c1, piece):
+            if piece == 0:
+                e_sb = work.tile([P, N], BF16, name="e_sb", tag="e_sb", bufs=4)
+                l3 = small.tile([P, 3], F32, name="l3", tag="l3")
+                e_t[i] = e_sb
+                l_t[i] = l3
+            nc.scalar.activation(
+                out=e_t[i][:, c0:c1], in_=ssb_t[i][:, c0:c1], func=ACT.Exp,
+                bias=nm_t[i][:, 0:1], scale=1.0, accum_out=l_t[i][:, piece : piece + 1],
+            )
 
         def lrec(i):
             rl = small.tile([P, 1], F32, name="rl", tag="rl")
             nc.vector.reciprocal(out=rl[:], in_=l_t[i][:])
             rl_t[i] = rl
 
-        def lrec_halves(i):
+        def lrec_pieces(i):
             l1 = small.tile([P, 1], F32, name="l1", tag="l1")
             nc.vector.tensor_reduce(out=l1[:], in_=l_t[i][:], axis=AX.X, op=ALU.add)
             rl = small.tile([P, 1], F32, name="rl", tag="rl")
             nc.vector.reciprocal(out=rl[:], in_=l1[:])
             rl_t[i] = rl
 
-        def tr(i, h):
-            tp = ps_t.tile([P, 4, P], F32, name="tp", tag="t")
+        def tr_words(i, h, q0, q1):
+            if q0 == 0:
+                if i < NB - 1:
+                    tp = ps_t.tile([P, 4, P], F32, name="tp", tag="t")
+                else:
+                    tp = ps_s.tile([P, 4, P], F32, name="tp", tag="s")
+                tp_t[(i, h)] = tp
             words = e_t[i][:].bitcast(F32)
-            for q in range(4):
+            for q in range(q0, q1):
                 w0 = (4 * h + q) * P
-                nc.tensor.transpose(tp[:, q, :], words[:, w0 : w0 + P], ident[:])
-            tp_t[(i, h)] = tp
+                nc.tensor.transpose(tp_t[(i, h)][:, q, :], words[:, w0 : w0 + P], ident[:])
 
-        def co(i, h, eng):
-            if h == 0:
+        def tr(i, h):
+            tr_words(i, h, 0, 4)
+
+        def co_words(i, h, g0, g1, eng):
+            if h == 0 and g0 == 0:
                 eg = work.tile([P, 4, P, 4], BF16, name="eg", tag="eg", bufs=4, align_bytes=64)
                 eg_t[i] = eg
             words = eg_t[i][:].rearrange("p g r t -> p (g r t)").bitcast(F32)
-            dst = words[:, 512 * h : 512 * (h + 1)].rearrange("p (g r v) -> p g r v", g=2, v=2)
-            src = tp_t[(i, h)][:].rearrange("p (g v) r -> p g r v", v=2)
+            dst = words[:, 512 * h + 256 * g0 : 512 * h + 256 * g1].rearrange("p (g r v) -> p g r v", g=g1 - g0, v=2)
+            src = tp_t[(i, h)][:, 2 * g0 : 2 * g1, :].rearrange("p (g v) r -> p g r v", v=2)
             if eng == "v":
                 nc.vector.tensor_copy(out=dst, in_=src)
             else:
                 nc.scalar.copy(out=dst, in_=src)
+
+        def co(i, h, eng):
+            co_words(i, h, 0, 2, eng)
 
         def quant_e(i):
             ec = work.tile([P, 512], U32, name="ec", tag="ec", bufs=4, align_bytes=64)
@@ -262,20 +272,20 @@ def tile_contranorm_pa_kernel(tc, x, out):
             )
             ec_t[i] = (ec, es)
 
-        def quant_e_half(i, h):
-            if h == 0:
+        def quant_e_groups(i, g0, g1):
+            if g0 == 0:
                 ec = work.tile([P, 512], U32, name="ec", tag="ec", bufs=4, align_bytes=64)
                 es = work.tile([P, 512], U8, name="es", tag="es", bufs=4, align_bytes=64)
                 ec_t[i] = (ec, es)
             ec, es = ec_t[i]
             nc.vector.quantize_mx(
-                out=ec[:, 256 * h : 256 * (h + 1)].bitcast(FP8X4), scales=es[:, 256 * h : 256 * (h + 1)],
-                in_=eg_t[i][:, 2 * h : 2 * h + 2, :, :].rearrange("p g r t -> p (g r t)"),
+                out=ec[:, P * g0 : P * g1].bitcast(FP8X4), scales=es[:, P * g0 : P * g1],
+                in_=eg_t[i][:, g0:g1, :, :].rearrange("p g r t -> p (g r t)"),
             )
 
         def mm2(i, g):
             if g == 0:
-                if i < NB - 4:
+                if i < NB - 2:
                     o_ps = ps_o.tile([P, D], F32, name="o_ps", tag="o")
                 else:
                     o_ps = ps_s.tile([P, D], F32, name="o_ps", tag="s")
@@ -378,9 +388,12 @@ def tile_contranorm_pa_kernel(tc, x, out):
                     mm2(k - 3, g)
             for n in range(4):
                 vmaxc(k + 2, n)
+            if k <= 2:
+                vnm(k + 2)
             if k >= 2:
                 quant_e(k - 2)
-            vnm(k + 2)
+            if not (k <= 2):
+                vnm(k + 2)
             if k == 1:
                 for g in (3, 0, 1, 2):
                     quant_x(g)
@@ -388,52 +401,56 @@ def tile_contranorm_pa_kernel(tc, x, out):
                 lrec(k - 1)
                 co(k - 1, 0, "s")
                 co(k - 1, 1, "s")
-            if k >= 3:
-                fin(k - 3, "s" if k < 8 else "v")
-            if k <= 2:
+            if 0 <= k - 4 < 7:
+                fin(k - 4, "s")
+            if k - 3 >= 7:
+                fin(k - 3, "v")
+            if k <= 5:
                 tr(k, 0)
                 tr(k, 1)
             if k + 3 < NB:
                 for n in range(4):
                     mm1(k + 3, n)
-            if not (k <= 2):
+            if not (k <= 5):
                 tr(k, 0)
                 tr(k, 1)
 
+        last = NB - 1
         expo(14)
         for g in range(4):
             mm2(11, g)
         quant_e(12)
+        for g in range(4):
+            mm2(12, g)
         co(13, 0, "v")
         lrec(13)
         co(13, 1, "v")
         tr(14, 0)
         tr(14, 1)
-        expo_halves(15)
+        expo_piece(15, 0, 1024, 0)
+        expo_piece(15, 1024, 1536, 1)
+        expo_piece(15, 1536, 2048, 2)
+        tr_words(15, 0, 0, 4)
         fin(11, "v")
         quant_e(13)
         for g in range(4):
-            mm2(12, g)
-        co(14, 0, "v")
-        lrec(14)
-        co(14, 1, "s")
-        tr(15, 0)
-        tr(15, 1)
-        for g in range(4):
             mm2(13, g)
-        co(15, 0, "v")
+        co(14, 0, "v")
+        co(14, 1, "v")
+        tr_words(15, 1, 0, 4)
+        co(15, 0, "s")
+        lrec(14)
         quant_e(14)
-        co(15, 1, "s")
-        quant_e_half(15, 0)
-        lrec_halves(15)
-        fin(12, "s")
         for g in range(4):
             mm2(14, g)
-        quant_e_half(15, 1)
-        fin(13, "v")
-        last = NB - 1
-        o_a = ps_o.tile([P, 256], F32, name="o_a", tag="o")
-        o_b = ps_s.tile([P, 256], F32, name="o_b", tag="s")
+        fin(12, "s")
+        quant_e_groups(15, 0, 2)
+        co_words(15, 1, 0, 2, "v")
+        lrec_pieces(15)
+        fin(13, "s")
+        quant_e_groups(15, 2, 4)
+        o_a = ps_s.tile([P, 256], F32, name="o_a", tag="s")
+        o_b = ps_o.tile([P, 256], F32, name="o_b", tag="o")
         ec, es = ec_t[last]
         for g in range(4):
             for o_half, c0 in ((o_a, 0), (o_b, 256)):

@@ -309,6 +309,11 @@ def tile_contranorm_pa_kernel(tc, x, out):
                 nc.scalar.activation(out=o_sb[:], in_=o_t[i][:], func=ACT.Copy, scale=rl_t[i][:, 0:1])
             nc.sync.dma_start(out=out[i * P : (i + 1) * P, :], in_=o_sb[:])
 
+        def keep_warm(count):
+            warm = ps_o.tile([P, 512], F32, name="warm", tag="o")
+            for r in range(count):
+                nc.tensor.matmul(out=warm[:], lhsT=x_sb[:, 0, 0:P], rhs=x_sb[:, 0, :], start=True, stop=True)
+
         squares_on_vector = (1, 3, 7)
 
         def sqs(b0, b1):
@@ -324,6 +329,7 @@ def tile_contranorm_pa_kernel(tc, x, out):
         tx_bank(0)
         xnorm(1)
         tx_bank(1)
+        keep_warm(3)
         cl(1)
         sqs(8, 9)
         rt(1)
@@ -335,6 +341,7 @@ def tile_contranorm_pa_kernel(tc, x, out):
         tx_bank(2)
         xnorm(3)
         tx_bank(3)
+        keep_warm(3)
         cl(2)
         sqs(12, 13)
         rt(2)
@@ -346,6 +353,7 @@ def tile_contranorm_pa_kernel(tc, x, out):
         tx_bank(4)
         xnorm(5)
         tx_bank(5)
+        keep_warm(4)
         cox(3, "v")
         cl(3)
         rt(3)

@@ -32,11 +32,11 @@ def tile_contranorm_pa_kernel(tc, x, out):
 
         ident = const.tile([P, P], F32, name="ident")
         x_sb = const.tile([P, NB, D], BF16, name="x_sb")
-        xc = const.tile([P, N], U32, name="xc", align_bytes=64)
-        xs = const.tile([P, N], U8, name="xs", align_bytes=64)
-        xqc = const.tile([P, 4 * D], U32, name="xqc", align_bytes=64)
-        xqs = const.tile([P, 4 * D], U8, name="xqs", align_bytes=64)
-        xg_3 = const.tile([P, D, 4], BF16, name="xg_3", align_bytes=64)
+        xc = const.tile([P, N], U32, name="xc", align_bytes=256)
+        xs = const.tile([P, N], U8, name="xs", align_bytes=256)
+        xqc = const.tile([P, 4 * D], U32, name="xqc", align_bytes=256)
+        xqs = const.tile([P, 4 * D], U8, name="xqs", align_bytes=256)
+        xg_3 = const.tile([P, D, 4], BF16, name="xg_3", align_bytes=256)
         ss = const.tile([P, NB], F32, name="ss")
         ssc = const.tile([P, NB], F32, name="ssc")
         nrm = const.tile([P, NB], F32, name="nrm")
@@ -107,9 +107,9 @@ def tile_contranorm_pa_kernel(tc, x, out):
             h = k % 2
             if h == 0:
                 if c < 3:
-                    xng = work.tile([P, 512, 4], BF16, name="xng", tag="xng", align_bytes=64)
+                    xng = work.tile([P, 512, 4], BF16, name="xng", tag="xng", align_bytes=256)
                 else:
-                    xng = work.tile([P, 512, 4], BF16, name="xng", tag="xlast", bufs=1, align_bytes=64)
+                    xng = work.tile([P, 512, 4], BF16, name="xng", tag="xlast", bufs=1, align_bytes=256)
                 xng_t[c] = xng
             words = xng_t[c][:].rearrange("p c t -> p (c t)").bitcast(F32)
             dst = words[:, 512 * h : 512 * (h + 1)].rearrange("p (r e v) -> p r e v", e=2, v=2)
@@ -140,9 +140,9 @@ def tile_contranorm_pa_kernel(tc, x, out):
 
         def regroup_x_gpsimd(g):
             if g == 0:
-                xg = work.tile([P, D, 4], BF16, name="xg", tag="xlast", bufs=1, align_bytes=64)
+                xg = work.tile([P, D, 4], BF16, name="xg", tag="xlast", bufs=1, align_bytes=256)
             else:
-                xg = work.tile([P, D, 4], BF16, name="xg", tag="xng", align_bytes=64)
+                xg = work.tile([P, D, 4], BF16, name="xg", tag="xng", align_bytes=256)
             xg_t[g] = xg
             nc.gpsimd.tensor_scalar(
                 out=xg[:], in0=x_sb[:, 4 * g : 4 * g + 4, :].rearrange("p t d -> p d t"),
@@ -251,7 +251,7 @@ def tile_contranorm_pa_kernel(tc, x, out):
 
         def co_words(i, h, g0, g1, eng):
             if h == 0 and g0 == 0:
-                eg = work.tile([P, 4, P, 4], BF16, name="eg", tag="eg", bufs=4, align_bytes=64)
+                eg = work.tile([P, 4, P, 4], BF16, name="eg", tag="eg", bufs=4, align_bytes=256)
                 eg_t[i] = eg
             words = eg_t[i][:].rearrange("p g r t -> p (g r t)").bitcast(F32)
             dst = words[:, 512 * h + 256 * g0 : 512 * h + 256 * g1].rearrange("p (g r v) -> p g r v", g=g1 - g0, v=2)
@@ -265,8 +265,8 @@ def tile_contranorm_pa_kernel(tc, x, out):
             co_words(i, h, 0, 2, eng)
 
         def quant_e(i):
-            ec = work.tile([P, 512], U32, name="ec", tag="ec", bufs=4, align_bytes=64)
-            es = work.tile([P, 512], U8, name="es", tag="es", bufs=4, align_bytes=64)
+            ec = work.tile([P, 512], U32, name="ec", tag="ec", bufs=4, align_bytes=256)
+            es = work.tile([P, 512], U8, name="es", tag="es", bufs=4, align_bytes=256)
             nc.vector.quantize_mx(
                 out=ec[:].bitcast(FP8X4), scales=es[:], in_=eg_t[i][:].rearrange("p g r t -> p (g r t)")
             )
@@ -274,8 +274,8 @@ def tile_contranorm_pa_kernel(tc, x, out):
 
         def quant_e_groups(i, g0, g1):
             if g0 == 0:
-                ec = work.tile([P, 512], U32, name="ec", tag="ec", bufs=4, align_bytes=64)
-                es = work.tile([P, 512], U8, name="es", tag="es", bufs=4, align_bytes=64)
+                ec = work.tile([P, 512], U32, name="ec", tag="ec", bufs=4, align_bytes=256)
+                es = work.tile([P, 512], U8, name="es", tag="es", bufs=4, align_bytes=256)
                 ec_t[i] = (ec, es)
             ec, es = ec_t[i]
             nc.vector.quantize_mx(

@@ -42,6 +42,7 @@ def tile_contranorm_pa_kernel(tc, x, out):
         nrm = const.tile([P, NB], F32, name="nrm")
         rn = const.tile([P, NB], F32, name="rn")
         one = const.tile([P, 1], F32, name="one")
+        minus_one = const.tile([P, 1], F32, name="minus_one")
         dmy = const.tile([P, 2], F32, name="dmy")
 
         x_v = x.rearrange("(u p e) d -> p u (e d)", p=P, e=2)
@@ -51,6 +52,7 @@ def tile_contranorm_pa_kernel(tc, x, out):
 
         nc.vector.memset(one[:], 1.0)
         make_identity(nc, ident[:])
+        nc.gpsimd.memset(minus_one[:], -1.0)
         nc.scalar.activation(out=dmy[:, 0:1], in_=one[:], func=ACT.Sqrt)
 
         xn_t = {}
@@ -197,6 +199,18 @@ def tile_contranorm_pa_kernel(tc, x, out):
             nc.vector.tensor_reduce(out=nm[:], in_=mx_t[i][:], axis=AX.X, op=ALU.max, negate=True)
             nm_t[i] = nm
 
+        def gnm(i):
+            top3 = small.tile([P, 1], F32, name="top3", tag="top3")
+            nm = small.tile([P, 1], F32, name="nm", tag="nm")
+            mx4 = mx_t[i]
+            nc.gpsimd.tensor_scalar(
+                out=top3[:], in0=mx4[:, 0:1], scalar1=mx4[:, 1:2], scalar2=mx4[:, 2:3], op0=ALU.max, op1=ALU.max
+            )
+            nc.gpsimd.tensor_scalar(
+                out=nm[:], in0=top3[:], scalar1=mx4[:, 3:4], scalar2=-1.0, op0=ALU.max, op1=ALU.mult
+            )
+            nm_t[i] = nm
+
         def vmax(i):
             for n in range(4):
                 vmaxc(i, n)
@@ -224,7 +238,7 @@ def tile_contranorm_pa_kernel(tc, x, out):
 
         def lrec(i):
             rl = small.tile([P, 1], F32, name="rl", tag="rl")
-            nc.vector.reciprocal(out=rl[:], in_=l_t[i][:])
+            nc.gpsimd.tensor_tensor(out=rl[:], in0=l_t[i][:], in1=minus_one[:], op=ALU.pow)
             rl_t[i] = rl
 
         def lrec_pieces(i):
@@ -396,22 +410,24 @@ def tile_contranorm_pa_kernel(tc, x, out):
                     mm2(k - 3, g)
             for n in range(4):
                 vmaxc(k + 2, n)
-            if k <= 2:
+            if k <= 1:
                 vnm(k + 2)
             if k >= 2:
                 quant_e(k - 2)
-            if not (k <= 2):
+            if 2 <= k < 4:
                 vnm(k + 2)
-            if k == 1:
+            if k >= 4:
+                gnm(k + 2)
+            if k == 2:
                 for g in (3, 0, 1, 2):
                     quant_x(g)
             if k >= 1:
                 lrec(k - 1)
                 co(k - 1, 0, "s")
                 co(k - 1, 1, "s")
-            if 0 <= k - 4 < 7:
+            if 0 <= k - 4 < 6:
                 fin(k - 4, "s")
-            if k - 3 >= 7:
+            if k - 3 >= 6:
                 fin(k - 3, "v")
             if k <= 5:
                 tr(k, 0)

@@ -36,7 +36,6 @@ def tile_contranorm_pa_kernel(tc, x, out):
         xs = const.tile([P, N], U8, name="xs", align_bytes=256)
         xqc = const.tile([P, 4 * D], U32, name="xqc", align_bytes=256)
         xqs = const.tile([P, 4 * D], U8, name="xqs", align_bytes=256)
-        xg_3 = const.tile([P, D, 4], BF16, name="xg_3", align_bytes=256)
         ss = const.tile([P, NB], F32, name="ss")
         ssc = const.tile([P, NB], F32, name="ssc")
         nrm = const.tile([P, NB], F32, name="nrm")
@@ -58,7 +57,7 @@ def tile_contranorm_pa_kernel(tc, x, out):
         xn_t = {}
         tx_t = {}
         xng_t = {}
-        xg_t = {3: xg_3}
+        xg_t = {}
 
         def sq(b, eng):
             if eng == "s":
@@ -135,16 +134,11 @@ def tile_contranorm_pa_kernel(tc, x, out):
                 in_=xng_t[c][:].rearrange("p c t -> p (c t)"),
             )
 
-        def regroup_x_scalar(g):
-            dst = xg_t[g][:].rearrange("p (c i) t -> p c t i", i=4)
-            src = x_sb[:, 4 * g : 4 * g + 4, :].rearrange("p t (c i) -> p c t i", i=4)
-            nc.scalar.copy(out=dst, in_=src)
-
         def regroup_x_gpsimd(g):
             if g == 0:
                 xg = work.tile([P, D, 4], BF16, name="xg", tag="xlast", bufs=1, align_bytes=256)
             else:
-                xg = work.tile([P, D, 4], BF16, name="xg", tag="xng", align_bytes=256)
+                xg = work.tile([P, D, 4], BF16, name="xg", tag="xg", bufs=3, align_bytes=256)
             xg_t[g] = xg
             nc.gpsimd.tensor_scalar(
                 out=xg[:], in0=x_sb[:, 4 * g : 4 * g + 4, :].rearrange("p t d -> p d t"),
@@ -367,39 +361,43 @@ def tile_contranorm_pa_kernel(tc, x, out):
         tx_bank(4)
         xnorm(5)
         tx_bank(5)
-        keep_warm(4)
+        keep_warm(3)
         cox(3, "v")
         cl(3)
         rt(3)
         quant_xn(1)
         rc(3)
+        mm1(0, 0)
+        mm1(0, 1)
         cox(4, "s")
         xnorm(6)
         tx_bank(6)
         xnorm(7)
         tx_bank(7)
-        mm1(0, 0)
-        mm1(0, 1)
+        vmaxc(0, 0)
         cox(5, "s")
         cox(6, "s")
         quant_xn(2)
-        vmaxc(0, 0)
         vmaxc(0, 1)
         mm1(0, 2)
         cox(7, "s")
+        mm1(1, 0)
         quant_xn(3)
-        vmaxc(0, 2)
         mm1(0, 3)
+        vmaxc(0, 2)
         vmaxc(0, 3)
         vnm(0)
+        vmaxc(1, 0)
         nc.scalar.activation(out=dmy[:, 1:2], in_=one[:], func=ACT.Exp)
-        regroup_x_scalar(3)
         regroup_x_gpsimd(0)
         regroup_x_gpsimd(1)
         regroup_x_gpsimd(2)
-        for n in range(4):
+        regroup_x_gpsimd(3)
+        for n in range(1, 4):
             mm1(1, n)
-        vmax(1)
+        for n in range(1, 4):
+            vmaxc(1, n)
+        vnm(1)
         for n in range(4):
             mm1(2, n)
 
@@ -419,7 +417,7 @@ def tile_contranorm_pa_kernel(tc, x, out):
             if k >= 4:
                 gnm(k + 2)
             if k == 2:
-                for g in (3, 0, 1, 2):
+                for g in range(4):
                     quant_x(g)
             if k >= 1:
                 lrec(k - 1)

@@ -423,9 +423,9 @@ def tile_contranorm_pa_kernel(tc, x, out):
                 lrec(k - 1)
                 co(k - 1, 0, "s")
                 co(k - 1, 1, "s")
-            if 0 <= k - 4 < 6:
+            if 0 <= k - 4 < 5:
                 fin(k - 4, "s")
-            if k - 3 >= 6:
+            if k - 3 >= 5:
                 fin(k - 3, "v")
             if k <= 5:
                 tr(k, 0)

from contextlib import ExitStack

import concourse.mybir as mybir
from concourse.masks import make_identity

F32 = mybir.dt.float32
BF16 = mybir.dt.bfloat16
U32 = mybir.dt.uint32
U8 = mybir.dt.uint8
FP8X4 = mybir.dt.float8_e4m3fn_x4
ALU = mybir.AluOpType
ACT = mybir.ActivationFunctionType
AX = mybir.AxisListType

P = 128
N = 2048
D = 512
NB = N // P
FLOPS = 2 * 2 * N * N * D


def tile_contranorm_pa_kernel(tc, x, out):
    nc = tc.nc
    with ExitStack() as ctx:
        const = ctx.enter_context(tc.tile_pool(name="const", bufs=1))
        work = ctx.enter_context(tc.tile_pool(name="work", bufs=2))
        small = ctx.enter_context(tc.tile_pool(name="small", bufs=8))
        ps_s = ctx.enter_context(tc.psum_pool(name="ps_s", bufs=4))
        ps_t = ctx.enter_context(tc.psum_pool(name="ps_t", bufs=2))
        ps_o = ctx.enter_context(tc.psum_pool(name="ps_o", bufs=2))
        ctx.enter_context(tc.manual_schedule())

        ident = const.tile([P, P], F32, name="ident")
        x_sb = const.tile([P, NB, D], BF16, name="x_sb")
        xc = const.tile([P, N], U32, name="xc", align_bytes=256)
        xs = const.tile([P, N], U8, name="xs", align_bytes=256)
        xqc = const.tile([P, 4 * D], U32, name="xqc", align_bytes=256)
        xqs = const.tile([P, 4 * D], U8, name="xqs", align_bytes=256)
        ss = const.tile([P, NB], F32, name="ss")
        ssc = const.tile([P, NB], F32, name="ssc")
        nrm = const.tile([P, NB], F32, name="nrm")
        rn = const.tile([P, NB], F32, name="rn")
        one = const.tile([P, 1], F32, name="one")
        minus_one = const.tile([P, 1], F32, name="minus_one")
        dmy = const.tile([P, 2], F32, name="dmy")

        x_v = x.rearrange("(u p e) d -> p u (e d)", p=P, e=2)
        x_sv = x_sb[:].rearrange("p (u e) d -> p u (e d)", e=2)
        for u0, u1 in ((0, 1), (1, 2), (2, 3), (3, 4), (4, 6), (6, 8)):
            nc.sync.dma_start(out=x_sv[:, u0:u1, :], in_=x_v[:, u0:u1, :])

        nc.vector.memset(one[:], 1.0)
        make_identity(nc, ident[:])
        nc.gpsimd.memset(minus_one[:], -1.0)
        nc.scalar.activation(out=dmy[:, 0:1], in_=one[:], func=ACT.Sqrt)

        xn_t = {}
        tx_t = {}
        xng_t = {}
        xg_t = {}

        def sq(b, eng):
            if eng == "s":
                junk_s = work.tile([P, D], BF16, name="junk_s", tag="junk_s")
                nc.scalar.activation(out=junk_s[:], in_=x_sb[:, b, :], func=ACT.Square, accum_out=ss[:, b : b + 1])
            else:
                junk_v = work.tile([P, D], F32, name="junk_v", tag="junk_v")
                nc.vector.scalar_tensor_tensor(
                    out=junk_v[:], in0=x_sb[:, b, :], scalar=1.0, in1=x_sb[:, b, :],
                    op0=ALU.mult, op1=ALU.mult, accum_out=ss[:, b : b + 1],
                )

        def cl(c):
            cols = slice(4 * c, 4 * c + 4)
            nc.vector.tensor_scalar_max(out=ssc[:, cols], in0=ss[:, cols], scalar1=1e-24)

        def rt(c):
            cols = slice(4 * c, 4 * c + 4)
            nc.scalar.activation(out=nrm[:, cols], in_=ssc[:, cols], func=ACT.Sqrt)

        def rc(c):
            cols = slice(4 * c, 4 * c + 4)
            nc.vector.reciprocal(out=rn[:, cols], in_=nrm[:, cols])

        def xnorm(u):
            xn = work.tile([P, 2, D], BF16, name="xn", tag="xn", bufs=8)
            for e in range(2):
                b = 2 * u + e
                nc.vector.tensor_scalar_mul(out=xn[:, e, :], in0=x_sb[:, b, :], scalar1=rn[:, b : b + 1])
            xn_t[u] = xn

        def tx_bank(k):
            if k < 4:
                tx = ps_s.tile([P, 2, 2, P], F32, name="tx", tag="s")
            elif k < 6:
                tx = ps_t.tile([P, 2, 2, P], F32, name="tx", tag="t")
            else:
                tx = ps_o.tile([P, 2, 2, P], F32, name="tx", tag="o")
            words = xn_t[k][:].rearrange("p a d -> p (a d)").bitcast(F32)
            for e in range(2):
                for v in range(2):
                    w0 = e * 256 + v * P
                    nc.tensor.transpose(tx[:, e, v, :], words[:, w0 : w0 + P], ident[:])
            tx_t[k] = tx

        def cox(k, eng):
            c = k // 2
            h = k % 2
            if h == 0:
                if c < 3:
                    xng = work.tile([P, 512, 4], BF16, name="xng", tag="xng", align_bytes=256)
                else:
                    xng = work.tile([P, 512, 4], BF16, name="xng", tag="xlast", bufs=1, align_bytes=256)
                xng_t[c] = xng
            words = xng_t[c][:].rearrange("p c t -> p (c t)").bitcast(F32)
            dst = words[:, 512 * h : 512 * (h + 1)].rearrange("p (r e v) -> p r e v", e=2, v=2)
            src = tx_t[k][:].rearrange("p e v r -> p r e v")
            if eng == "v":
                nc.vector.tensor_copy(out=dst, in_=src)
            else:
                nc.scalar.copy(out=dst, in_=src)

        def quant_xn_half(c, h):
            nc.vector.quantize_mx(
                out=xc[:, 512 * c + 256 * h : 512 * c + 256 * (h + 1)].bitcast(FP8X4),
                scales=xs[:, 512 * c + 256 * h : 512 * c + 256 * (h + 1)],
                in_=xng_t[c][:, 256 * h : 256 * (h + 1), :].rearrange("p c t -> p (c t)"),
            )

        def quant_xn(c):
            nc.vector.quantize_mx(
                out=xc[:, 512 * c : 512 * (c + 1)].bitcast(FP8X4),
                scales=xs[:, 512 * c : 512 * (c + 1)],
                in_=xng_t[c][:].rearrange("p c t -> p (c t)"),
            )

        def regroup_x_gpsimd(g):
            if g == 0:
                xg = work.tile([P, D, 4], BF16, name="xg", tag="xlast", bufs=1, align_bytes=256)
            else:
                xg = work.tile([P, D, 4], BF16, name="xg", tag="xg", bufs=3, align_bytes=256)
            xg_t[g] = xg
            nc.gpsimd.tensor_scalar(
                out=xg[:], in0=x_sb[:, 4 * g : 4 * g + 4, :].rearrange("p t d -> p d t"),
                scalar1=1.0, scalar2=0.0, op0=ALU.mult, op1=ALU.add,
            )

        def quant_x(g):
            nc.vector.quantize_mx(
                out=xqc[:, D * g : D * (g + 1)].bitcast(FP8X4),
                scales=xqs[:, D * g : D * (g + 1)],
                in_=xg_t[g][:].rearrange("p d t -> p (d t)"),
            )

        s_t = {}
        ssb_t = {}
        mx_t = {}
        nm_t = {}
        e_t = {}
        l_t = {}
        rl_t = {}
        tp_t = {}
        eg_t = {}
        ec_t = {}
        o_t = {}

        def mm1(i, n):
            s = ps_s.tile([P, 512], F32, name="s", tag="s")
            nc.tensor.matmul_mx(
                out=s[:],
                lhsT=xc[:, i * P : (i + 1) * P].bitcast(FP8X4),
                lhsT_scale=xs[:, i * P : (i + 1) * P],
                rhs=xc[:, n * 512 : (n + 1) * 512].bitcast(FP8X4),
                rhs_scale=xs[:, n * 512 : (n + 1) * 512],
                start=True,
                stop=True,
            )
            s_t[(i, n)] = s

        def vmaxc(i, n):
            if n == 0:
                s_sb = work.tile([P, N], F32, name="s_sb", tag="s_sb", bufs=4)
                mx4 = small.tile([P, 4], F32, name="mx4", tag="mx4")
                ssb_t[i] = s_sb
                mx_t[i] = mx4
            nc.vector.tensor_scalar(
                out=ssb_t[i][:, n * 512 : (n + 1) * 512], in0=s_t[(i, n)][:], scalar1=1.0, scalar2=None,
                op0=ALU.mult, op1=ALU.max, accum_out=mx_t[i][:, n : n + 1],
            )

        def vnm(i):
            nm = small.tile([P, 1], F32, name="nm", tag="nm")
            nc.vector.tensor_reduce(out=nm[:], in_=mx_t[i][:], axis=AX.X, op=ALU.max, negate=True)
            nm_t[i] = nm

        def gnm(i):
            top3 = small.tile([P, 1], F32, name="top3", tag="top3")
            nm = small.tile([P, 1], F32, name="nm", tag="nm")
            mx4 = mx_t[i]
            nc.gpsimd.tensor_scalar(
                out=top3[:], in0=mx4[:, 0:1], scalar1=mx4[:, 1:2], scalar2=mx4[:, 2:3], op0=ALU.max, op1=ALU.max
            )
            nc.gpsimd.tensor_scalar(
                out=nm[:], in0=top3[:], scalar1=mx4[:, 3:4], scalar2=-1.0, op0=ALU.max, op1=ALU.mult
            )
            nm_t[i] = nm

        def vmax(i):
            for n in range(4):
                vmaxc(i, n)
            vnm(i)

        def expo(i):
            e_sb = work.tile([P, N], BF16, name="e_sb", tag="e_sb", bufs=4)
            l1 = small.tile([P, 1], F32, name="l1", tag="l1")
            nc.scalar.activation(
                out=e_sb[:], in_=ssb_t[i][:], func=ACT.Exp, bias=nm_t[i][:, 0:1], scale=1.0, accum_out=l1[:, 0:1]
            )
            e_t[i] = e_sb
            l_t[i] = l1

        def expo_piece(i, c0, c1, piece):
            if piece == 0:
                e_sb = work.tile([P, N], BF16, name="e_sb", tag="e_sb", bufs=4)
                l3 = small.tile([P, 3], F32, name="l3", tag="l3")
                e_t[i] = e_sb
                l_t[i] = l3
            nc.scalar.activation(
                out=e_t[i][:, c0:c1], in_=ssb_t[i][:, c0:c1], func=ACT.Exp,
                bias=nm_t[i][:, 0:1], scale=1.0, accum_out=l_t[i][:, piece : piece + 1],
            )

        def lrec(i):
            rl = small.tile([P, 1], F32, name="rl", tag="rl")
            nc.gpsimd.tensor_tensor(out=rl[:], in0=l_t[i][:], in1=minus_one[:], op=ALU.pow)
            rl_t[i] = rl

        def lrec_pieces(i):
            l1 = small.tile([P, 1], F32, name="l1", tag="l1")
            nc.vector.tensor_reduce(out=l1[:], in_=l_t[i][:], axis=AX.X, op=ALU.add)
            rl = small.tile([P, 1], F32, name="rl", tag="rl")
            nc.vector.reciprocal(out=rl[:], in_=l1[:])
            rl_t[i] = rl

        def tr_words(i, h, q0, q1):
            if q0 == 0:
                if i < NB - 1:
                    tp = ps_t.tile([P, 4, P], F32, name="tp", tag="t")
                else:
                    tp = ps_s.tile([P, 4, P], F32, name="tp", tag="s")
                tp_t[(i, h)] = tp
            words = e_t[i][:].bitcast(F32)
            for q in range(q0, q1):
                w0 = (4 * h + q) * P
                nc.tensor.transpose(tp_t[(i, h)][:, q, :], words[:, w0 : w0 + P], ident[:])

        def tr(i, h):
            tr_words(i, h, 0, 4)

        def co_words(i, h, g0, g1, eng):
            if h == 0 and g0 == 0:
                eg = work.tile([P, 4, P, 4], BF16, name="eg", tag="eg", bufs=4, align_bytes=256)
                eg_t[i] = eg
            words = eg_t[i][:].rearrange("p g r t -> p (g r t)").bitcast(F32)
            dst = words[:, 512 * h + 256 * g0 : 512 * h + 256 * g1].rearrange("p (g r v) -> p g r v", g=g1 - g0, v=2)
            src = tp_t[(i, h)][:, 2 * g0 : 2 * g1, :].rearrange("p (g v) r -> p g r v", v=2)
            if eng == "v":
                nc.vector.tensor_copy(out=dst, in_=src)
            else:
                nc.scalar.copy(out=dst, in_=src)

        def co(i, h, eng):
            co_words(i, h, 0, 2, eng)

        def quant_e(i):
            ec = work.tile([P, 512], U32, name="ec", tag="ec", bufs=4, align_bytes=256)
            es = work.tile([P, 512], U8, name="es", tag="es", bufs=4, align_bytes=256)
            nc.vector.quantize_mx(
                out=ec[:].bitcast(FP8X4), scales=es[:], in_=eg_t[i][:].rearrange("p g r t -> p (g r t)")
            )
            ec_t[i] = (ec, es)

        def quant_e_groups(i, g0, g1):
            if g0 == 0:
                ec = work.tile([P, 512], U32, name="ec", tag="ec", bufs=4, align_bytes=256)
                es = work.tile([P, 512], U8, name="es", tag="es", bufs=4, align_bytes=256)
                ec_t[i] = (ec, es)
            ec, es = ec_t[i]
            nc.vector.quantize_mx(
                out=ec[:, P * g0 : P * g1].bitcast(FP8X4), scales=es[:, P * g0 : P * g1],
                in_=eg_t[i][:, g0:g1, :, :].rearrange("p g r t -> p (g r t)"),
            )

        def mm2(i, g):
            if g == 0:
                if i < NB - 2:
                    o_ps = ps_o.tile([P, D], F32, name="o_ps", tag="o")
                else:
                    o_ps = ps_s.tile([P, D], F32, name="o_ps", tag="s")
                o_t[i] = o_ps
            ec, es = ec_t[i]
            nc.tensor.matmul_mx(
                out=o_t[i][:],
                lhsT=ec[:, g * P : (g + 1) * P].bitcast(FP8X4),
                lhsT_scale=es[:, g * P : (g + 1) * P],
                rhs=xqc[:, g * D : (g + 1) * D].bitcast(FP8X4),
                rhs_scale=xqs[:, g * D : (g + 1) * D],
                start=(g == 0),
                stop=(g == 3),
            )

        def fin(i, eng):
            o_sb = work.tile([P, D], F32, name="o_sb", tag="o_sb", bufs=4)
            if eng == "v":
                nc.vector.tensor_scalar_mul(out=o_sb[:], in0=o_t[i][:], scalar1=rl_t[i][:, 0:1])
            else:
                nc.scalar.activation(out=o_sb[:], in_=o_t[i][:], func=ACT.Copy, scale=rl_t[i][:, 0:1])
            nc.sync.dma_start(out=out[i * P : (i + 1) * P, :], in_=o_sb[:])

        def keep_warm(count):
            warm = ps_o.tile([P, 512], F32, name="warm", tag="o")
            for r in range(count):
                nc.tensor.matmul(out=warm[:], lhsT=x_sb[:, 0, 0:P], rhs=x_sb[:, 0, :], start=True, stop=True)

        squares_on_vector = (1, 3, 7)

        def sqs(b0, b1):
            for b in range(b0, b1):
                sq(b, "v" if b in squares_on_vector else "s")

        sqs(0, 5)
        cl(0)
        rt(0)
        sqs(5, 8)
        rc(0)
        xnorm(0)
        tx_bank(0)
        xnorm(1)
        tx_bank(1)
        keep_warm(3)
        cl(1)
        sqs(8, 9)
        rt(1)
        cox(0, "v")
        sqs(9, 12)
        rc(1)
        cox(1, "v")
        xnorm(2)
        tx_bank(2)
        xnorm(3)
        tx_bank(3)
        keep_warm(3)
        cl(2)
        sqs(12, 13)
        rt(2)
        quant_xn(0)
        sqs(13, 16)
        rc(2)
        cox(2, "v")
        xnorm(4)
        tx_bank(4)
        xnorm(5)
        tx_bank(5)
        keep_warm(3)
        cox(3, "v")
        cl(3)
        rt(3)
        quant_xn(1)
        rc(3)
        mm1(0, 0)
        mm1(0, 1)
        cox(4, "s")
        xnorm(6)
        tx_bank(6)
        xnorm(7)
        tx_bank(7)
        vmaxc(0, 0)
        cox(5, "s")
        cox(6, "s")
        quant_xn(2)
        vmaxc(0, 1)
        mm1(0, 2)
        cox(7, "s")
        mm1(1, 0)
        quant_xn(3)
        mm1(0, 3)
        vmaxc(0, 2)
        vmaxc(0, 3)
        vnm(0)
        vmaxc(1, 0)
        nc.scalar.activation(out=dmy[:, 1:2], in_=one[:], func=ACT.Exp)
        regroup_x_gpsimd(0)
        regroup_x_gpsimd(1)
        regroup_x_gpsimd(2)
        regroup_x_gpsimd(3)
        for n in range(1, 4):
            mm1(1, n)
        for n in range(1, 4):
            vmaxc(1, n)
        vnm(1)
        for n in range(4):
            mm1(2, n)

        for k in range(NB - 2):
            expo(k)
            if k >= 3:
                for g in range(4):
                    mm2(k - 3, g)
            for n in range(4):
                vmaxc(k + 2, n)
            if k <= 1:
                vnm(k + 2)
            if k >= 2:
                quant_e(k - 2)
            if 2 <= k < 4:
                vnm(k + 2)
            if k >= 4:
                gnm(k + 2)
            if k == 2:
                for g in range(4):
                    quant_x(g)
            if k >= 1:
                lrec(k - 1)
                co(k - 1, 0, "s")
                co(k - 1, 1, "s")
            if 0 <= k - 4 < 5:
                fin(k - 4, "s")
            if k - 3 >= 5:
                fin(k - 3, "v")
            if k <= 5:
                tr(k, 0)
                tr(k, 1)
            if k + 3 < NB:
                for n in range(4):
                    mm1(k + 3, n)
            if not (k <= 5):
                tr(k, 0)
                tr(k, 1)

        last = NB - 1
        expo(14)
        for g in range(4):
            mm2(11, g)
        quant_e(12)
        for g in range(4):
            mm2(12, g)
        co(13, 0, "v")
        lrec(13)
        co(13, 1, "v")
        tr(14, 0)
        tr(14, 1)
        expo_piece(15, 0, 1024, 0)
        expo_piece(15, 1024, 1536, 1)
        expo_piece(15, 1536, 2048, 2)
        tr_words(15, 0, 0, 4)
        fin(11, "v")
        quant_e(13)
        for g in range(4):
            mm2(13, g)
        co(14, 0, "v")
        co(14, 1, "v")
        tr_words(15, 1, 0, 4)
        co(15, 0, "s")
        lrec(14)
        quant_e(14)
        for g in range(4):
            mm2(14, g)
        fin(12, "s")
        quant_e_groups(15, 0, 2)
        co_words(15, 1, 0, 2, "v")
        lrec_pieces(15)
        fin(13, "s")
        quant_e_groups(15, 2, 4)
        o_a = ps_s.tile([P, 256], F32, name="o_a", tag="s")
        o_b = ps_o.tile([P, 256], F32, name="o_b", tag="o")
        ec, es = ec_t[last]
        for g in range(4):
            for o_half, c0 in ((o_a, 0), (o_b, 256)):
                nc.tensor.matmul_mx(
                    out=o_half[:],
                    lhsT=ec[:, g * P : (g + 1) * P].bitcast(FP8X4),
                    lhsT_scale=es[:, g * P : (g + 1) * P],
                    rhs=xqc[:, g * D + c0 : g * D + c0 + 256].bitcast(FP8X4),
                    rhs_scale=xqs[:, g * D + c0 : g * D + c0 + 256],
                    start=(g == 0),
                    stop=(g == 3),
                )
        fin(last - 1, "s")
        oa_sb = work.tile([P, 256], F32, name="oa_sb", tag="oa_sb", bufs=1)
        ob_sb = work.tile([P, 256], F32, name="ob_sb", tag="ob_sb", bufs=1)
        nc.vector.tensor_scalar_mul(out=oa_sb[:], in0=o_a[:], scalar1=rl_t[last][:, 0:1])
        nc.scalar.activation(out=ob_sb[:], in_=o_b[:], func=ACT.Copy, scale=rl_t[last][:, 0:1])
        nc.sync.dma_start(out=out[last * P : (last + 1) * P, 0:256], in_=oa_sb[:])
        nc.scalar.dma_start(out=out[last * P : (last + 1) * P, 256:512], in_=ob_sb[:])
